import numpy as np
import ml_dtypes


def mxq(x, axis, fmt="e4m3"):
    dtype, down = {"e4m3": (ml_dtypes.float8_e4m3fn, 7), "e5m2": (ml_dtypes.float8_e5m2, 14)}[fmt]
    v = np.moveaxis(np.asarray(x, np.float32).astype(ml_dtypes.bfloat16).astype(np.float64), axis, -1)
    blocks = v.reshape(v.shape[:-1] + (-1, 32))
    amax = np.abs(blocks).max(-1, keepdims=True)
    byte = np.maximum(np.where(amax > 0, np.frexp(amax)[1] - 1 + 127, 0) - down, 1)
    scale = np.exp2(byte - 127.0)
    codes = (blocks / scale).astype(np.float32).astype(dtype).astype(np.float64)
    return np.moveaxis((codes * scale).reshape(v.shape), -1, axis)


WIDE = False


def mx_kscale(k):
    if not WIDE:
        return np.ones(k)
    levels = np.array([10, -10, 5, -5, 0])
    if k % 512:
        return np.exp2(np.random.permutation(np.resize(levels, k // 32))).repeat(32)
    a = np.empty((k // 512, 16))
    for p in range(k // 512):
        a[p, :8] = np.random.permutation(np.resize(levels, 8))
        for g in range(8):
            far = levels[np.abs(levels - a[p, g]) >= 10]
            a[p, g + 8] = far[np.random.randint(len(far))]
    return np.exp2(a.ravel()).repeat(32)


BF16 = ml_dtypes.bfloat16


def bf(x):
    return np.asarray(x, np.float32).astype(BF16)


def f64(x):
    return np.asarray(x).astype(np.float64)


B, T, C, KW = 2, 1024, 512, 3
PAD = KW // 2


def setup_inputs():
    s = mx_kscale(C)
    return {"x": bf(np.random.standard_normal((B, T, C)) * s),
            "w1": bf(np.random.standard_normal((C, C)) / np.sqrt(C) / s[None, :]),
            "b1": bf(np.random.standard_normal(C) * 0.2),
            "w2": bf(np.random.standard_normal((C, KW)) * 0.8),
            "b2": bf(np.random.standard_normal(C) * 0.2)}


def core(x, w1, b1, w2, b2):
    h = (mxq(f64(x), 2, "e4m3") @ mxq(f64(w1), 1, "e4m3").T) + f64(b1)
    hp = np.pad(h, ((0, 0), (PAD, PAD), (0, 0)))
    taps = f64(w2)
    y = hp[:, 0:T, :] * taps[:, 0]
    for j in range(1, KW):
        y = y + hp[:, j:j + T, :] * taps[:, j]
    return y + f64(b2)


def e4m3fn_bytes(y):
    return np.clip(np.asarray(y, np.float64), -448.0, 448.0).astype(np.float32).astype(ml_dtypes.float8_e4m3fn).view(np.uint8)


Y_SCALE = 140.0


def reference(x, w1, b1, w2, b2):
    out = core(x, w1, b1, w2, b2)
    return out, e4m3fn_bytes(out * Y_SCALE)

@@ -1,0 +1,176 @@
+from contextlib import ExitStack
+
+import concourse.mybir as mybir
+from concourse.masks import make_identity
+
+B, T, C, D, KW = 2, 1024, 512, 512, 3
+Y_SCALE = 140.0
+FLOPS = 2 * B * T * C * D + 2 * KW * B * T * D
+
+F32 = mybir.dt.float32
+BF16 = mybir.dt.bfloat16
+U32 = mybir.dt.uint32
+U8 = mybir.dt.uint8
+FP8X4 = mybir.dt.float8_e4m3fn_x4
+FP8 = mybir.dt.float8_e4m3fn
+ALU = mybir.AluOpType
+ACT = mybir.ActivationFunctionType
+
+P = 128
+ND = D // P
+WORDS = C // 2
+
+WINDOWS = [(0, 0, 512), (0, 512, 512), (1, 0, 512), (1, 512, 512)]
+
+
+def tile_cvim_pa_kernel(tc, x, w1, b1, w2, b2, out_0, out_1):
+    nc = tc.nc
+    o0 = out_0.flatten_outer_dims()
+    o1 = out_1.flatten_outer_dims()
+
+    with ExitStack() as ctx:
+        const = ctx.enter_context(tc.tile_pool(name="const", bufs=1))
+        xin = ctx.enter_context(tc.tile_pool(name="xin", bufs=len(WINDOWS)))
+        grp = ctx.enter_context(tc.tile_pool(name="grp", bufs=2))
+        cod = ctx.enter_context(tc.tile_pool(name="cod", bufs=3))
+        res = ctx.enter_context(tc.tile_pool(name="res", bufs=4))
+        ps_in = ctx.enter_context(tc.psum_pool(name="ps_in", bufs=2))
+        ps_acc = ctx.enter_context(tc.psum_pool(name="ps_acc", bufs=4))
+        ps_out = ctx.enter_context(tc.psum_pool(name="ps_out", bufs=2))
+
+        w_raw = const.tile([P, ND, C], BF16, name="w_raw")
+        w_view = w1.rearrange("(j p) c -> p j c", p=P)
+        nc.sync.dma_start(out=w_raw[:, 0:2, :], in_=w_view[:, 0:2, :])
+        nc.sync.dma_start(out=w_raw[:, 2:4, :], in_=w_view[:, 2:4, :])
+        x_raw = []
+        for b, t0, n in WINDOWS:
+            xr = xin.tile([P, n // P, C], BF16, name="xr")
+            nc.sync.dma_start(out=xr[:], in_=x[b, t0 : t0 + n, :].rearrange("(n p) c -> p n c", p=P))
+            x_raw.append(xr)
+
+        w2_b = const.tile([P, ND, KW], BF16, name="w2_b")
+        b1_b = const.tile([P, ND], BF16, name="b1_b")
+        b2_b = const.tile([P, ND], BF16, name="b2_b")
+        with nc.allow_non_contiguous_dma(reason="one value of a 512-long vector to a partition"):
+            nc.scalar.dma_start(out=w2_b[:], in_=w2.rearrange("(j p) k -> p j k", p=P))
+            nc.scalar.dma_start(out=b1_b[:], in_=b1.rearrange("(j p) -> p j", p=P))
+            nc.scalar.dma_start(out=b2_b[:], in_=b2.rearrange("(j p) -> p j", p=P))
+
+        warm = const.tile([P, 1], F32, name="warm")
+        nc.vector.memset(warm[:], 0.0)
+        nc.scalar.activation(out=warm[:], in_=warm[:], func=ACT.Identity)
+
+        ident = const.tile([P, P], F32, name="ident")
+        make_identity(nc, ident[:])
+
+        taps = const.tile([P, ND, KW], F32, name="taps")
+        nc.gpsimd.tensor_copy(out=taps[:], in_=w2_b[:])
+        beta = const.tile([P, ND], F32, name="beta")
+        beta_first = const.tile([P, ND], F32, name="beta_first")
+        beta_last = const.tile([P, ND], F32, name="beta_last")
+        edge = const.tile([P, ND], F32, name="edge")
+        nc.gpsimd.tensor_tensor(out=beta[:], in0=taps[:, :, 0], in1=taps[:, :, 1], op=ALU.add)
+        nc.gpsimd.tensor_tensor(out=beta[:], in0=beta[:], in1=taps[:, :, 2], op=ALU.add)
+        nc.gpsimd.tensor_tensor(out=beta[:], in0=beta[:], in1=b1_b[:], op=ALU.mult)
+        nc.gpsimd.tensor_tensor(out=beta[:], in0=beta[:], in1=b2_b[:], op=ALU.add)
+        nc.gpsimd.tensor_tensor(out=edge[:], in0=taps[:, :, 0], in1=b1_b[:], op=ALU.mult)
+        nc.gpsimd.tensor_tensor(out=beta_first[:], in0=beta[:], in1=edge[:], op=ALU.subtract)
+        edge2 = const.tile([P, ND], F32, name="edge2")
+        nc.gpsimd.tensor_tensor(out=edge2[:], in0=taps[:, :, 2], in1=b1_b[:], op=ALU.mult)
+        nc.gpsimd.tensor_tensor(out=beta_last[:], in0=beta[:], in1=edge2[:], op=ALU.subtract)
+
+        y = []
+        for b in range(B):
+            yb = const.tile([P, ND, T], F32, name="y%d" % b)
+            nc.gpsimd.tensor_copy(out=yb[:, :, 0:1], in_=beta_first[:].unsqueeze(2))
+            y.append(yb)
+
+        def to_mx(raw, nt, codes, scales, engines):
+            words = raw[:].bitcast(F32)
+            grouped = grp.tile([P, nt * P * 4], BF16, name="grouped", align_bytes=64)
+            g_words = grouped[:].bitcast(F32)
+            for h in range(0, nt, 2):
+                na = min(2, nt - h)
+                turned = ps_in.tile([P, 2, 2, P], F32, name="turned")
+                for a in range(na):
+                    for u in range(2):
+                        nc.tensor.transpose(out=turned[:, a, u, :], in_=words[:, h + a, u:WORDS:2], identity=ident[:])
+                dst = g_words[:, 2 * P * h : 2 * P * (h + na)].rearrange("p (a r u) -> p a r u", a=na, u=2)
+                src = turned[:, 0:na].rearrange("p a u r -> p a r u")
+                if engines[(h // 2) % len(engines)] == "v":
+                    nc.vector.tensor_copy(out=dst, in_=src)
+                else:
+                    nc.scalar.copy(out=dst, in_=src)
+            nc.vector.quantize_mx(out=codes.bitcast(FP8X4), scales=scales, in_=grouped[:])
+
+        w_codes = const.tile([P, D], U32, name="w_codes", align_bytes=64)
+        w_scales = const.tile([P, D], U8, name="w_scales", align_bytes=64)
+        to_mx(w_raw, ND, w_codes[:], w_scales[:], "vs")
+
+        x_mx = {}
+
+        def stage_in(i):
+            n = WINDOWS[i][2]
+            x_codes = cod.tile([P, n], U32, name="x_codes", align_bytes=64)
+            x_scales = cod.tile([P, n], U8, name="x_scales", align_bytes=64)
+            to_mx(x_raw[i], n // P, x_codes[:], x_scales[:], "vs" if i == 0 else "s")
+            x_mx[i] = (x_codes, x_scales)
+
+        def stage_mm(i):
+            b, t0, n = WINDOWS[i]
+            x_codes, x_scales = x_mx[i]
+            for j in range(ND):
+                acc = ps_acc.tile([P, n], F32, name="acc")
+                nc.tensor.matmul_mx(
+                    out=acc[:],
+                    lhsT=w_codes[:, j * P : (j + 1) * P].bitcast(FP8X4),
+                    lhsT_scale=w_scales[:, j * P : (j + 1) * P],
+                    rhs=x_codes[:].bitcast(FP8X4),
+                    rhs_scale=x_scales[:],
+                    start=True,
+                    stop=True,
+                )
+                yj = y[b][:, j, :]
+                m = n if t0 + n < T else n - 2
+                nc.scalar.activation(
+                    out=yj[:, t0 + 1 : t0 + 1 + m], in_=acc[:, 0:m], func=ACT.Identity,
+                    bias=beta[:, j : j + 1], scale=taps[:, j, 0:1],
+                )
+                if t0 + n == T:
+                    nc.scalar.activation(
+                        out=yj[:, T - 1 : T], in_=acc[:, n - 2 : n - 1], func=ACT.Identity,
+                        bias=beta_last[:, j : j + 1], scale=taps[:, j, 0:1],
+                    )
+                nc.vector.scalar_tensor_tensor(
+                    out=yj[:, t0 : t0 + n], in0=acc[:], scalar=taps[:, j, 1:2], in1=yj[:, t0 : t0 + n],
+                    op0=ALU.mult, op1=ALU.add,
+                )
+                lo = 1 if t0 == 0 else 0
+                nc.vector.scalar_tensor_tensor(
+                    out=yj[:, t0 + lo - 1 : t0 + n - 1], in0=acc[:, lo:n], scalar=taps[:, j, 2:3],
+                    in1=yj[:, t0 + lo - 1 : t0 + n - 1], op0=ALU.mult, op1=ALU.add,
+                )
+
+        def stage_out(b, k):
+            turned_y = ps_out.tile([P, D], F32, name="turned_y")
+            for j in range(ND):
+                nc.tensor.transpose(out=turned_y[:, j * P : (j + 1) * P], in_=y[b][:, j, k * P : (k + 1) * P], identity=ident[:])
+            r32 = res.tile([P, D], F32, name="r32")
+            nc.scalar.copy(out=r32[:], in_=turned_y[:])
+            r8 = res.tile([P, D], FP8, name="r8")
+            nc.vector.tensor_scalar(out=r8[:], in0=r32[:], scalar1=Y_SCALE, scalar2=None, op0=ALU.mult, saturate=False)
+            rows = slice(b * T + k * P, b * T + (k + 1) * P)
+            nc.sync.dma_start(out=o0[rows, :], in_=r32[:])
+            nc.sync.dma_start(out=o1[rows, :], in_=r8[:].bitcast(U8))
+
+        done = {0: 0, 1: 0}
+        stage_in(0)
+        for i in range(len(WINDOWS)):
+            if i + 1 < len(WINDOWS):
+                stage_in(i + 1)
+            stage_mm(i)
+            b, t0, n = WINDOWS[i]
+            ready = T // P if t0 + n == T else (t0 + n - 1) // P
+            for k in range(done[b], ready):
+                stage_out(b, k)
+            done[b] = ready

@@ -20,33 +20,25 @@ P = 128
 ND = D // P
 WORDS = C // 2
 
-WINDOWS = [(0, 0, 512), (0, 512, 512), (1, 0, 512), (1, 512, 512)]
+WINDOWS = [(0, 0, 256), (0, 256, 256), (0, 512, 512), (1, 0, 512), (1, 512, 256), (1, 768, 128), (1, 896, 128)]
+IN_LEAD = 8
+OUT_LEAD = 1
+SCALAR_CASTS = 8
 
 
 def tile_cvim_pa_kernel(tc, x, w1, b1, w2, b2, out_0, out_1):
     nc = tc.nc
     o0 = out_0.flatten_outer_dims()
     o1 = out_1.flatten_outer_dims()
+    NW = len(WINDOWS)
 
     with ExitStack() as ctx:
         const = ctx.enter_context(tc.tile_pool(name="const", bufs=1))
-        xin = ctx.enter_context(tc.tile_pool(name="xin", bufs=len(WINDOWS)))
-        grp = ctx.enter_context(tc.tile_pool(name="grp", bufs=2))
-        cod = ctx.enter_context(tc.tile_pool(name="cod", bufs=3))
-        res = ctx.enter_context(tc.tile_pool(name="res", bufs=4))
-        ps_in = ctx.enter_context(tc.psum_pool(name="ps_in", bufs=2))
-        ps_acc = ctx.enter_context(tc.psum_pool(name="ps_acc", bufs=4))
-        ps_out = ctx.enter_context(tc.psum_pool(name="ps_out", bufs=2))
-
-        w_raw = const.tile([P, ND, C], BF16, name="w_raw")
-        w_view = w1.rearrange("(j p) c -> p j c", p=P)
-        nc.sync.dma_start(out=w_raw[:, 0:2, :], in_=w_view[:, 0:2, :])
-        nc.sync.dma_start(out=w_raw[:, 2:4, :], in_=w_view[:, 2:4, :])
-        x_raw = []
-        for b, t0, n in WINDOWS:
-            xr = xin.tile([P, n // P, C], BF16, name="xr")
-            nc.sync.dma_start(out=xr[:], in_=x[b, t0 : t0 + n, :].rearrange("(n p) c -> p n c", p=P))
-            x_raw.append(xr)
+        xin = ctx.enter_context(tc.tile_pool(name="xin", bufs=NW))
+        grp = ctx.enter_context(tc.tile_pool(name="grp", bufs=3))
+        cod = ctx.enter_context(tc.tile_pool(name="cod", bufs=NW))
+        res = ctx.enter_context(tc.tile_pool(name="res", bufs=6))
+        psum = ctx.enter_context(tc.psum_pool(name="psum", bufs=8))
 
         w2_b = const.tile([P, ND, KW], BF16, name="w2_b")
         b1_b = const.tile([P, ND], BF16, name="b1_b")
@@ -55,6 +47,22 @@ def tile_cvim_pa_kernel(tc, x, w1, b1, w2, b2, out_0, out_1):
             nc.scalar.dma_start(out=w2_b[:], in_=w2.rearrange("(j p) k -> p j k", p=P))
             nc.scalar.dma_start(out=b1_b[:], in_=b1.rearrange("(j p) -> p j", p=P))
             nc.scalar.dma_start(out=b2_b[:], in_=b2.rearrange("(j p) -> p j", p=P))
+
+        w_raw = const.tile([P, ND, C], BF16, name="w_raw")
+        w_view = w1.rearrange("(j p) c -> p j c", p=P)
+        x_raw = []
+
+        def load_x(i):
+            b, t0, n = WINDOWS[i]
+            xr = xin.tile([P, n // P, C], BF16, name="xr")
+            nc.sync.dma_start(out=xr[:], in_=x[b, t0 : t0 + n, :].rearrange("(n p) c -> p n c", p=P))
+            x_raw.append(xr)
+
+        nc.sync.dma_start(out=w_raw[:, 0:2, :], in_=w_view[:, 0:2, :])
+        load_x(0)
+        nc.sync.dma_start(out=w_raw[:, 2:4, :], in_=w_view[:, 2:4, :])
+        for i in range(1, NW):
+            load_x(i)
 
         warm = const.tile([P, 1], F32, name="warm")
         nc.vector.memset(warm[:], 0.0)
@@ -69,43 +77,43 @@ def tile_cvim_pa_kernel(tc, x, w1, b1, w2, b2, out_0, out_1):
         beta_first = const.tile([P, ND], F32, name="beta_first")
         beta_last = const.tile([P, ND], F32, name="beta_last")
         edge = const.tile([P, ND], F32, name="edge")
+        edge2 = const.tile([P, ND], F32, name="edge2")
         nc.gpsimd.tensor_tensor(out=beta[:], in0=taps[:, :, 0], in1=taps[:, :, 1], op=ALU.add)
         nc.gpsimd.tensor_tensor(out=beta[:], in0=beta[:], in1=taps[:, :, 2], op=ALU.add)
         nc.gpsimd.tensor_tensor(out=beta[:], in0=beta[:], in1=b1_b[:], op=ALU.mult)
         nc.gpsimd.tensor_tensor(out=beta[:], in0=beta[:], in1=b2_b[:], op=ALU.add)
         nc.gpsimd.tensor_tensor(out=edge[:], in0=taps[:, :, 0], in1=b1_b[:], op=ALU.mult)
         nc.gpsimd.tensor_tensor(out=beta_first[:], in0=beta[:], in1=edge[:], op=ALU.subtract)
-        edge2 = const.tile([P, ND], F32, name="edge2")
-        nc.gpsimd.tensor_tensor(out=edge2[:], in0=taps[:, :, 2], in1=b1_b[:], op=ALU.mult)
-        nc.gpsimd.tensor_tensor(out=beta_last[:], in0=beta[:], in1=edge2[:], op=ALU.subtract)
 
         y = []
         for b in range(B):
             yb = const.tile([P, ND, T], F32, name="y%d" % b)
             nc.gpsimd.tensor_copy(out=yb[:, :, 0:1], in_=beta_first[:].unsqueeze(2))
             y.append(yb)
+        nc.gpsimd.tensor_tensor(out=edge2[:], in0=taps[:, :, 2], in1=b1_b[:], op=ALU.mult)
+        nc.gpsimd.tensor_tensor(out=beta_last[:], in0=beta[:], in1=edge2[:], op=ALU.subtract)
 
-        def to_mx(raw, nt, codes, scales, engines):
-            words = raw[:].bitcast(F32)
+        def to_mx(words, nt, codes, scales):
             grouped = grp.tile([P, nt * P * 4], BF16, name="grouped", align_bytes=64)
             g_words = grouped[:].bitcast(F32)
             for h in range(0, nt, 2):
                 na = min(2, nt - h)
-                turned = ps_in.tile([P, 2, 2, P], F32, name="turned")
+                bank = psum.tile([P, 512], F32, name="bank")
+                turned = bank[:].rearrange("p (a u r) -> p a u r", a=2, u=2)
                 for a in range(na):
                     for u in range(2):
                         nc.tensor.transpose(out=turned[:, a, u, :], in_=words[:, h + a, u:WORDS:2], identity=ident[:])
                 dst = g_words[:, 2 * P * h : 2 * P * (h + na)].rearrange("p (a r u) -> p a r u", a=na, u=2)
-                src = turned[:, 0:na].rearrange("p a u r -> p a r u")
-                if engines[(h // 2) % len(engines)] == "v":
-                    nc.vector.tensor_copy(out=dst, in_=src)
-                else:
-                    nc.scalar.copy(out=dst, in_=src)
+                nc.scalar.copy(out=dst, in_=turned[:, 0:na].rearrange("p a u r -> p a r u"))
             nc.vector.quantize_mx(out=codes.bitcast(FP8X4), scales=scales, in_=grouped[:])
 
         w_codes = const.tile([P, D], U32, name="w_codes", align_bytes=64)
         w_scales = const.tile([P, D], U8, name="w_scales", align_bytes=64)
-        to_mx(w_raw, ND, w_codes[:], w_scales[:], "vs")
+        w_words = w_raw[:].bitcast(F32)
+
+        def stage_w(half):
+            cols = slice(half * 2 * P, (half + 1) * 2 * P)
+            to_mx(w_words[:, 2 * half : 2 * half + 2, :], 2, w_codes[:, cols], w_scales[:, cols])
 
         x_mx = {}
 
@@ -113,64 +121,120 @@ def tile_cvim_pa_kernel(tc, x, w1, b1, w2, b2, out_0, out_1):
             n = WINDOWS[i][2]
             x_codes = cod.tile([P, n], U32, name="x_codes", align_bytes=64)
             x_scales = cod.tile([P, n], U8, name="x_scales", align_bytes=64)
-            to_mx(x_raw[i], n // P, x_codes[:], x_scales[:], "vs" if i == 0 else "s")
+            to_mx(x_raw[i][:].bitcast(F32), n // P, x_codes[:], x_scales[:])
             x_mx[i] = (x_codes, x_scales)
 
-        def stage_mm(i):
-            b, t0, n = WINDOWS[i]
+        units = [(i, j) for i in range(NW) for j in range(ND)]
+        NU = len(units)
+        accs = {}
+
+        def unit_mm(s):
+            i, j = units[s]
+            n = WINDOWS[i][2]
             x_codes, x_scales = x_mx[i]
-            for j in range(ND):
-                acc = ps_acc.tile([P, n], F32, name="acc")
-                nc.tensor.matmul_mx(
-                    out=acc[:],
-                    lhsT=w_codes[:, j * P : (j + 1) * P].bitcast(FP8X4),
-                    lhsT_scale=w_scales[:, j * P : (j + 1) * P],
-                    rhs=x_codes[:].bitcast(FP8X4),
-                    rhs_scale=x_scales[:],
-                    start=True,
-                    stop=True,
-                )
-                yj = y[b][:, j, :]
-                m = n if t0 + n < T else n - 2
-                nc.scalar.activation(
-                    out=yj[:, t0 + 1 : t0 + 1 + m], in_=acc[:, 0:m], func=ACT.Identity,
-                    bias=beta[:, j : j + 1], scale=taps[:, j, 0:1],
-                )
-                if t0 + n == T:
-                    nc.scalar.activation(
-                        out=yj[:, T - 1 : T], in_=acc[:, n - 2 : n - 1], func=ACT.Identity,
-                        bias=beta_last[:, j : j + 1], scale=taps[:, j, 0:1],
-                    )
-                nc.vector.scalar_tensor_tensor(
-                    out=yj[:, t0 : t0 + n], in0=acc[:], scalar=taps[:, j, 1:2], in1=yj[:, t0 : t0 + n],
-                    op0=ALU.mult, op1=ALU.add,
-                )
-                lo = 1 if t0 == 0 else 0
-                nc.vector.scalar_tensor_tensor(
-                    out=yj[:, t0 + lo - 1 : t0 + n - 1], in0=acc[:, lo:n], scalar=taps[:, j, 2:3],
-                    in1=yj[:, t0 + lo - 1 : t0 + n - 1], op0=ALU.mult, op1=ALU.add,
-                )
+            bank = psum.tile([P, 512], F32, name="bank")
+            nc.tensor.matmul_mx(
+                out=bank[:, 0:n],
+                lhsT=w_codes[:, j * P : (j + 1) * P].bitcast(FP8X4),
+                lhsT_scale=w_scales[:, j * P : (j + 1) * P],
+                rhs=x_codes[:].bitcast(FP8X4),
+                rhs_scale=x_scales[:],
+                start=True,
+                stop=True,
+            )
+            accs[s] = bank
 
-        def stage_out(b, k):
-            turned_y = ps_out.tile([P, D], F32, name="turned_y")
-            for j in range(ND):
-                nc.tensor.transpose(out=turned_y[:, j * P : (j + 1) * P], in_=y[b][:, j, k * P : (k + 1) * P], identity=ident[:])
-            r32 = res.tile([P, D], F32, name="r32")
-            nc.scalar.copy(out=r32[:], in_=turned_y[:])
-            r8 = res.tile([P, D], FP8, name="r8")
-            nc.vector.tensor_scalar(out=r8[:], in0=r32[:], scalar1=Y_SCALE, scalar2=None, op0=ALU.mult, saturate=False)
-            rows = slice(b * T + k * P, b * T + (k + 1) * P)
-            nc.sync.dma_start(out=o0[rows, :], in_=r32[:])
-            nc.sync.dma_start(out=o1[rows, :], in_=r8[:].bitcast(U8))
-
-        done = {0: 0, 1: 0}
-        stage_in(0)
-        for i in range(len(WINDOWS)):
-            if i + 1 < len(WINDOWS):
-                stage_in(i + 1)
-            stage_mm(i)
+        def unit_prev(s):
+            i, j = units[s]
             b, t0, n = WINDOWS[i]
-            ready = T // P if t0 + n == T else (t0 + n - 1) // P
-            for k in range(done[b], ready):
-                stage_out(b, k)
-            done[b] = ready
+            acc = accs[s]
+            yj = y[b][:, j, :]
+            m = n if t0 + n < T else n - 2
+            nc.scalar.activation(
+                out=yj[:, t0 + 1 : t0 + 1 + m], in_=acc[:, 0:m], func=ACT.Identity,
+                bias=beta[:, j : j + 1], scale=taps[:, j, 0:1],
+            )
+            if t0 + n == T:
+                nc.scalar.activation(
+                    out=yj[:, T - 1 : T], in_=acc[:, n - 2 : n - 1], func=ACT.Identity,
+                    bias=beta_last[:, j : j + 1], scale=taps[:, j, 0:1],
+                )
+
+        def unit_mid(s):
+            i, j = units[s]
+            b, t0, n = WINDOWS[i]
+            yj = y[b][:, j, :]
+            nc.vector.scalar_tensor_tensor(
+                out=yj[:, t0 : t0 + n], in0=accs[s][:, 0:n], scalar=taps[:, j, 1:2], in1=yj[:, t0 : t0 + n],
+                op0=ALU.mult, op1=ALU.add,
+            )
+
+        def unit_next(s):
+            i, j = units[s]
+            b, t0, n = WINDOWS[i]
+            yj = y[b][:, j, :]
+            lo = 1 if t0 == 0 else 0
+            nc.vector.scalar_tensor_tensor(
+                out=yj[:, t0 + lo - 1 : t0 + n - 1], in0=accs[s][:, lo:n], scalar=taps[:, j, 2:3],
+                in1=yj[:, t0 + lo - 1 : t0 + n - 1], op0=ALU.mult, op1=ALU.add,
+            )
+
+        def tile_out(b, k, by_scalar, cast_later):
+            bank = psum.tile([P, 512], F32, name="bank")
+            for j in range(ND):
+                nc.tensor.transpose(out=bank[:, j * P : (j + 1) * P], in_=y[b][:, j, k * P : (k + 1) * P], identity=ident[:])
+            rows = slice(b * T + k * P, b * T + (k + 1) * P)
+            r32 = res.tile([P, D], F32, name="r32")
+            r8 = res.tile([P, D], FP8, name="r8")
+            nc.scalar.copy(out=r32[:], in_=bank[:])
+            nc.sync.dma_start(out=o0[rows, :], in_=r32[:])
+
+            def cast():
+                if by_scalar:
+                    nc.scalar.activation(out=r8[:], in_=bank[:], func=ACT.Copy, scale=Y_SCALE, saturate=False)
+                else:
+                    nc.vector.tensor_scalar(out=r8[:], in0=r32[:], scalar1=Y_SCALE, scalar2=None, op0=ALU.mult, saturate=False)
+                nc.sync.dma_start(out=o1[rows, :], in_=r8[:].bitcast(U8))
+
+            if by_scalar:
+                cast()
+            else:
+                cast_later(cast)
+
+        first = -2
+        early = {}
+        for i in range(NW):
+            early.setdefault(max(first, ND * i - IN_LEAD), []).append(i)
+        late = {}
+        done = {0: 0, 1: 0}
+        n_out = [0]
+
+        stage_w(0)
+        for s in range(first, NU + 16):
+            for i in early.get(s, []):
+                stage_in(i)
+                if i == 0:
+                    stage_w(1)
+            if 0 <= s + 2 < NU:
+                unit_mm(s + 2)
+            if 0 <= s + 1 < NU:
+                unit_prev(s + 1)
+            if 0 <= s < NU:
+                unit_mid(s)
+            if 0 <= s - 1 < NU:
+                unit_next(s - 1)
+                i, j = units[s - 1]
+                b, t0, n = WINDOWS[i]
+                if j == ND - 1:
+                    ready = T // P if t0 + n == T else (t0 + n - 1) // P
+                    for r, k in enumerate(range(done[b], ready)):
+                        late.setdefault(s + OUT_LEAD + r, []).append((b, k))
+                    done[b] = ready
+            for item in late.get(s, []):
+                if len(item) == 1:
+                    item[0]()
+                else:
+                    b, k = item
+                    by_scalar = n_out[0] % SCALAR_CASTS == SCALAR_CASTS - 3
+                    n_out[0] += 1
+                    tile_out(b, k, by_scalar, lambda fn: late.setdefault(s + 1, []).append((fn,)))

@@ -15,15 +15,25 @@ FP8X4 = mybir.dt.float8_e4m3fn_x4
 FP8 = mybir.dt.float8_e4m3fn
 ALU = mybir.AluOpType
 ACT = mybir.ActivationFunctionType
+AX = mybir.AxisListType
 
 P = 128
 ND = D // P
 WORDS = C // 2
 
 WINDOWS = [(0, 0, 256), (0, 256, 256), (0, 512, 512), (1, 0, 512), (1, 512, 256), (1, 768, 128), (1, 896, 128)]
+HEAD_STAGES = [[("w", 0), ("w", 1)], [("x", 0, 0), ("x", 0, 1)], [("w", 2), ("w", 3)]]
+HEAD_WINDOWS = (0,)
+HEAD_ENGINES = ("s", "s", "s")
 IN_LEAD = 8
+ONE_ONE = 1.0019454956054688
+KICK = 14
+KICK_HEAD = 4
+MM_LEAD = 3
 OUT_LEAD = 1
-SCALAR_CASTS = 8
+SCALAR_CASTS = (5, 13)
+DIAG = (0, 3)
+VECTOR_COPIES = ()
 
 
 def tile_cvim_pa_kernel(tc, x, w1, b1, w2, b2, out_0, out_1):
@@ -34,9 +44,7 @@ def tile_cvim_pa_kernel(tc, x, w1, b1, w2, b2, out_0, out_1):
 
     with ExitStack() as ctx:
         const = ctx.enter_context(tc.tile_pool(name="const", bufs=1))
-        xin = ctx.enter_context(tc.tile_pool(name="xin", bufs=NW))
         grp = ctx.enter_context(tc.tile_pool(name="grp", bufs=3))
-        cod = ctx.enter_context(tc.tile_pool(name="cod", bufs=NW))
         res = ctx.enter_context(tc.tile_pool(name="res", bufs=6))
         psum = ctx.enter_context(tc.psum_pool(name="psum", bufs=8))
 
@@ -48,19 +56,25 @@ def tile_cvim_pa_kernel(tc, x, w1, b1, w2, b2, out_0, out_1):
             nc.scalar.dma_start(out=b1_b[:], in_=b1.rearrange("(j p) -> p j", p=P))
             nc.scalar.dma_start(out=b2_b[:], in_=b2.rearrange("(j p) -> p j", p=P))
 
-        w_raw = const.tile([P, ND, C], BF16, name="w_raw")
         w_view = w1.rearrange("(j p) c -> p j c", p=P)
-        x_raw = []
+        w_raw = {}
+        x_raw = {}
+
+        def load_w(j0, j1):
+            wr = const.tile([P, j1 - j0, C], BF16, name="w_raw%d" % j0)
+            nc.sync.dma_start(out=wr[:], in_=w_view[:, j0:j1, :])
+            for j in range(j0, j1):
+                w_raw[j] = wr[:, j - j0, :]
 
         def load_x(i):
             b, t0, n = WINDOWS[i]
-            xr = xin.tile([P, n // P, C], BF16, name="xr")
+            xr = const.tile([P, n // P, C], BF16, name="x_raw%d" % i)
             nc.sync.dma_start(out=xr[:], in_=x[b, t0 : t0 + n, :].rearrange("(n p) c -> p n c", p=P))
-            x_raw.append(xr)
+            x_raw[i] = xr
 
-        nc.sync.dma_start(out=w_raw[:, 0:2, :], in_=w_view[:, 0:2, :])
+        load_w(0, 2)
         load_x(0)
-        nc.sync.dma_start(out=w_raw[:, 2:4, :], in_=w_view[:, 2:4, :])
+        load_w(2, 4)
         for i in range(1, NW):
             load_x(i)
 
@@ -68,32 +82,59 @@ def tile_cvim_pa_kernel(tc, x, w1, b1, w2, b2, out_0, out_1):
         nc.vector.memset(warm[:], 0.0)
         nc.scalar.activation(out=warm[:], in_=warm[:], func=ACT.Identity)
 
+        ones = const.tile([P, 512], BF16, name="ones", align_bytes=64)
+        ones_codes = const.tile([P, P], U32, name="ones_codes", align_bytes=64)
+        ones_scales = const.tile([P, P], U8, name="ones_scales", align_bytes=64)
+        nc.vector.memset(ones[:].bitcast(F32), ONE_ONE)
+        nc.vector.quantize_mx(out=ones_codes[:].bitcast(FP8X4), scales=ones_scales[:], in_=ones[:])
+        idle = psum.tile([P, 512], F32, name="bank")
+
+        def kick(times):
+            for r in range(times):
+                nc.tensor.matmul_mx(
+                    out=idle[:, 0:P], lhsT=ones_codes[:].bitcast(FP8X4), lhsT_scale=ones_scales[:],
+                    rhs=ones_codes[:].bitcast(FP8X4), rhs_scale=ones_scales[:], start=True, stop=True,
+                )
+
+        kick(KICK)
+
         ident = const.tile([P, P], F32, name="ident")
         make_identity(nc, ident[:])
 
         taps = const.tile([P, ND, KW], F32, name="taps")
-        nc.gpsimd.tensor_copy(out=taps[:], in_=w2_b[:])
+        nc.vector.tensor_copy(out=taps[:], in_=w2_b[:])
         beta = const.tile([P, ND], F32, name="beta")
         beta_first = const.tile([P, ND], F32, name="beta_first")
-        beta_last = const.tile([P, ND], F32, name="beta_last")
-        edge = const.tile([P, ND], F32, name="edge")
+        edge0 = const.tile([P, ND], F32, name="edge0")
         edge2 = const.tile([P, ND], F32, name="edge2")
-        nc.gpsimd.tensor_tensor(out=beta[:], in0=taps[:, :, 0], in1=taps[:, :, 1], op=ALU.add)
-        nc.gpsimd.tensor_tensor(out=beta[:], in0=beta[:], in1=taps[:, :, 2], op=ALU.add)
-        nc.gpsimd.tensor_tensor(out=beta[:], in0=beta[:], in1=b1_b[:], op=ALU.mult)
-        nc.gpsimd.tensor_tensor(out=beta[:], in0=beta[:], in1=b2_b[:], op=ALU.add)
-        nc.gpsimd.tensor_tensor(out=edge[:], in0=taps[:, :, 0], in1=b1_b[:], op=ALU.mult)
-        nc.gpsimd.tensor_tensor(out=beta_first[:], in0=beta[:], in1=edge[:], op=ALU.subtract)
+        nc.vector.tensor_reduce(out=beta[:], in_=taps[:], op=ALU.add, axis=AX.X)
+        nc.vector.tensor_tensor(out=edge0[:], in0=taps[:, :, 0], in1=b1_b[:], op=ALU.mult)
+        nc.vector.tensor_tensor(out=beta[:], in0=beta[:], in1=b1_b[:], op=ALU.mult)
+        nc.vector.tensor_tensor(out=edge2[:], in0=taps[:, :, 2], in1=b1_b[:], op=ALU.mult)
+        nc.vector.tensor_tensor(out=beta[:], in0=beta[:], in1=b2_b[:], op=ALU.add)
+        nc.vector.tensor_tensor(out=beta_first[:], in0=beta[:], in1=edge0[:], op=ALU.subtract)
 
         y = []
         for b in range(B):
             yb = const.tile([P, ND, T], F32, name="y%d" % b)
-            nc.gpsimd.tensor_copy(out=yb[:, :, 0:1], in_=beta_first[:].unsqueeze(2))
+            nc.vector.tensor_copy(out=yb[:, :, 0:1], in_=beta_first[:].unsqueeze(2))
             y.append(yb)
-        nc.gpsimd.tensor_tensor(out=edge2[:], in0=taps[:, :, 2], in1=b1_b[:], op=ALU.mult)
-        nc.gpsimd.tensor_tensor(out=beta_last[:], in0=beta[:], in1=edge2[:], op=ALU.subtract)
 
-        def to_mx(words, nt, codes, scales):
+        hpad = const.tile([P, T + 2], F32, name="hpad")
+        nc.vector.memset(hpad[:, 0:1], 0.0)
+        nc.vector.memset(hpad[:, T + 1 : T + 2], 0.0)
+        b1_f = const.tile([P, ND], F32, name="b1_f")
+        nc.vector.tensor_copy(out=b1_f[:], in_=b1_b[:])
+        diag = const.tile([P, KW, P], F32, name="diag")
+        for r in range(KW):
+            nc.vector.tensor_scalar(out=diag[:, r, :], in0=ident[:], scalar1=taps[:, DIAG[1], r : r + 1], scalar2=None, op0=ALU.mult)
+        b2_rep = const.tile([P, P], F32, name="b2_rep")
+        nc.vector.tensor_copy(out=b2_rep[:], in_=b2_b[:, DIAG[1] : DIAG[1] + 1].to_broadcast([P, P]))
+
+        def to_mx(slots, name, engine):
+            nt = len(slots)
+            codes = const.tile([P, nt * P], U32, name="codes_" + name, align_bytes=64)
+            scales = const.tile([P, nt * P], U8, name="scales_" + name, align_bytes=64)
             grouped = grp.tile([P, nt * P * 4], BF16, name="grouped", align_bytes=64)
             g_words = grouped[:].bitcast(F32)
             for h in range(0, nt, 2):
@@ -102,27 +143,39 @@ def tile_cvim_pa_kernel(tc, x, w1, b1, w2, b2, out_0, out_1):
                 turned = bank[:].rearrange("p (a u r) -> p a u r", a=2, u=2)
                 for a in range(na):
                     for u in range(2):
-                        nc.tensor.transpose(out=turned[:, a, u, :], in_=words[:, h + a, u:WORDS:2], identity=ident[:])
+                        nc.tensor.transpose(out=turned[:, a, u, :], in_=slots[h + a][:, u:WORDS:2], identity=ident[:])
                 dst = g_words[:, 2 * P * h : 2 * P * (h + na)].rearrange("p (a r u) -> p a r u", a=na, u=2)
-                nc.scalar.copy(out=dst, in_=turned[:, 0:na].rearrange("p a u r -> p a r u"))
-            nc.vector.quantize_mx(out=codes.bitcast(FP8X4), scales=scales, in_=grouped[:])
+                if engine == "v":
+                    nc.vector.tensor_copy(out=dst, in_=turned[:, 0:na].rearrange("p a u r -> p a r u"))
+                else:
+                    nc.scalar.copy(out=dst, in_=turned[:, 0:na].rearrange("p a u r -> p a r u"))
+            nc.vector.quantize_mx(out=codes[:].bitcast(FP8X4), scales=scales[:], in_=grouped[:])
+            return codes, scales
 
-        w_codes = const.tile([P, D], U32, name="w_codes", align_bytes=64)
-        w_scales = const.tile([P, D], U8, name="w_scales", align_bytes=64)
-        w_words = w_raw[:].bitcast(F32)
-
-        def stage_w(half):
-            cols = slice(half * 2 * P, (half + 1) * 2 * P)
-            to_mx(w_words[:, 2 * half : 2 * half + 2, :], 2, w_codes[:, cols], w_scales[:, cols])
-
+        w_mx = {}
         x_mx = {}
+
+        def stage_head(q):
+            slots = []
+            for item in HEAD_STAGES[q]:
+                if item[0] == "w":
+                    slots.append(w_raw[item[1]].bitcast(F32))
+                else:
+                    slots.append(x_raw[item[1]][:, item[2], :].bitcast(F32))
+            codes, scales = to_mx(slots, "h%d" % q, HEAD_ENGINES[q])
+            for a, item in enumerate(HEAD_STAGES[q]):
+                cols = slice(a * P, (a + 1) * P)
+                if item[0] == "w":
+                    w_mx[item[1]] = (codes[:, cols], scales[:, cols])
+                elif item[2] == 0:
+                    n = WINDOWS[item[1]][2]
+                    x_mx[item[1]] = (codes[:, a * P : a * P + n], scales[:, a * P : a * P + n])
 
         def stage_in(i):
             n = WINDOWS[i][2]
-            x_codes = cod.tile([P, n], U32, name="x_codes", align_bytes=64)
-            x_scales = cod.tile([P, n], U8, name="x_scales", align_bytes=64)
-            to_mx(x_raw[i][:].bitcast(F32), n // P, x_codes[:], x_scales[:])
-            x_mx[i] = (x_codes, x_scales)
+            xw = x_raw[i][:].bitcast(F32)
+            codes, scales = to_mx([xw[:, a, :] for a in range(n // P)], "x%d" % i, "s")
+            x_mx[i] = (codes[:], scales[:])
 
         units = [(i, j) for i in range(NW) for j in range(ND)]
         NU = len(units)
@@ -132,13 +185,14 @@ def tile_cvim_pa_kernel(tc, x, w1, b1, w2, b2, out_0, out_1):
             i, j = units[s]
             n = WINDOWS[i][2]
             x_codes, x_scales = x_mx[i]
+            w_codes, w_scales = w_mx[j]
             bank = psum.tile([P, 512], F32, name="bank")
             nc.tensor.matmul_mx(
                 out=bank[:, 0:n],
-                lhsT=w_codes[:, j * P : (j + 1) * P].bitcast(FP8X4),
-                lhsT_scale=w_scales[:, j * P : (j + 1) * P],
-                rhs=x_codes[:].bitcast(FP8X4),
-                rhs_scale=x_scales[:],
+                lhsT=w_codes.bitcast(FP8X4),
+                lhsT_scale=w_scales,
+                rhs=x_codes.bitcast(FP8X4),
+                rhs_scale=x_scales,
                 start=True,
                 stop=True,
             )
@@ -147,22 +201,23 @@ def tile_cvim_pa_kernel(tc, x, w1, b1, w2, b2, out_0, out_1):
         def unit_prev(s):
             i, j = units[s]
             b, t0, n = WINDOWS[i]
-            acc = accs[s]
-            yj = y[b][:, j, :]
-            m = n if t0 + n < T else n - 2
+            if (b, j) == DIAG:
+                nc.scalar.activation(
+                    out=hpad[:, 1 + t0 : 1 + t0 + n], in_=accs[s][:, 0:n], func=ACT.Identity,
+                    bias=b1_f[:, j : j + 1], scale=1.0,
+                )
+                return
+            m = n if t0 + n < T else n - 1
             nc.scalar.activation(
-                out=yj[:, t0 + 1 : t0 + 1 + m], in_=acc[:, 0:m], func=ACT.Identity,
+                out=y[b][:, j, t0 + 1 : t0 + 1 + m], in_=accs[s][:, 0:m], func=ACT.Identity,
                 bias=beta[:, j : j + 1], scale=taps[:, j, 0:1],
             )
-            if t0 + n == T:
-                nc.scalar.activation(
-                    out=yj[:, T - 1 : T], in_=acc[:, n - 2 : n - 1], func=ACT.Identity,
-                    bias=beta_last[:, j : j + 1], scale=taps[:, j, 0:1],
-                )
 
         def unit_mid(s):
             i, j = units[s]
             b, t0, n = WINDOWS[i]
+            if (b, j) == DIAG:
+                return
             yj = y[b][:, j, :]
             nc.vector.scalar_tensor_tensor(
                 out=yj[:, t0 : t0 + n], in0=accs[s][:, 0:n], scalar=taps[:, j, 1:2], in1=yj[:, t0 : t0 + n],
@@ -172,6 +227,8 @@ def tile_cvim_pa_kernel(tc, x, w1, b1, w2, b2, out_0, out_1):
         def unit_next(s):
             i, j = units[s]
             b, t0, n = WINDOWS[i]
+            if (b, j) == DIAG:
+                return
             yj = y[b][:, j, :]
             lo = 1 if t0 == 0 else 0
             nc.vector.scalar_tensor_tensor(
@@ -179,14 +236,30 @@ def tile_cvim_pa_kernel(tc, x, w1, b1, w2, b2, out_0, out_1):
                 in1=yj[:, t0 + lo - 1 : t0 + n - 1], op0=ALU.mult, op1=ALU.add,
             )
 
-        def tile_out(b, k, by_scalar, cast_later):
+        def last_column(b):
+            nj = DIAG[1] if b == DIAG[0] else ND
+            col = y[b][:, 0:nj, T - 1 : T]
+            nc.vector.tensor_tensor(out=col, in0=col, in1=edge2[:, 0:nj].unsqueeze(2), op=ALU.subtract)
+
+        def tile_out(b, k, by_scalar, by_vector, cast_later):
             bank = psum.tile([P, 512], F32, name="bank")
             for j in range(ND):
-                nc.tensor.transpose(out=bank[:, j * P : (j + 1) * P], in_=y[b][:, j, k * P : (k + 1) * P], identity=ident[:])
+                if (b, j) == DIAG:
+                    nc.tensor.matmul(out=bank[:, j * P : (j + 1) * P], lhsT=b2_rep[:], rhs=ident[:], is_transpose=True, start=True, stop=False)
+                    for r in range(KW):
+                        nc.tensor.matmul(
+                            out=bank[:, j * P : (j + 1) * P], lhsT=hpad[:, k * P + r : (k + 1) * P + r], rhs=diag[:, r, :],
+                            start=False, stop=(r == KW - 1),
+                        )
+                else:
+                    nc.tensor.transpose(out=bank[:, j * P : (j + 1) * P], in_=y[b][:, j, k * P : (k + 1) * P], identity=ident[:])
             rows = slice(b * T + k * P, b * T + (k + 1) * P)
             r32 = res.tile([P, D], F32, name="r32")
             r8 = res.tile([P, D], FP8, name="r8")
-            nc.scalar.copy(out=r32[:], in_=bank[:])
+            if by_vector:
+                nc.vector.tensor_copy(out=r32[:], in_=bank[:])
+            else:
+                nc.scalar.copy(out=r32[:], in_=bank[:])
             nc.sync.dma_start(out=o0[rows, :], in_=r32[:])
 
             def cast():
@@ -201,30 +274,45 @@ def tile_cvim_pa_kernel(tc, x, w1, b1, w2, b2, out_0, out_1):
             else:
                 cast_later(cast)
 
-        first = -2
+        first = -MM_LEAD
         early = {}
         for i in range(NW):
-            early.setdefault(max(first, ND * i - IN_LEAD), []).append(i)
+            if i not in HEAD_WINDOWS:
+                early.setdefault(max(first, ND * i - IN_LEAD), []).append(i)
         late = {}
         done = {0: 0, 1: 0}
         n_out = [0]
 
-        stage_w(0)
+        for q in range(len(HEAD_STAGES)):
+            stage_head(q)
+            kick(KICK_HEAD)
         for s in range(first, NU + 16):
             for i in early.get(s, []):
                 stage_in(i)
-                if i == 0:
-                    stage_w(1)
-            if 0 <= s + 2 < NU:
-                unit_mm(s + 2)
+            if 0 <= s + MM_LEAD < NU:
+                unit_mm(s + MM_LEAD)
             if 0 <= s + 1 < NU:
                 unit_prev(s + 1)
             if 0 <= s < NU:
-                unit_mid(s)
+                i, j = units[s]
+                b, t0, n = WINDOWS[i]
+                if i == NW - 1:
+                    unit_next(s)
+                    if j == ND - 1:
+                        for r, k in enumerate(range(done[b], t0 // P)):
+                            late.setdefault(s + OUT_LEAD + r, []).append((b, k))
+                        done[b] = t0 // P
+                else:
+                    unit_mid(s)
             if 0 <= s - 1 < NU:
-                unit_next(s - 1)
                 i, j = units[s - 1]
                 b, t0, n = WINDOWS[i]
+                if j == ND - 1 and t0 + n == T:
+                    last_column(b)
+                if i == NW - 1:
+                    unit_mid(s - 1)
+                else:
+                    unit_next(s - 1)
                 if j == ND - 1:
                     ready = T // P if t0 + n == T else (t0 + n - 1) // P
                     for r, k in enumerate(range(done[b], ready)):
@@ -235,6 +323,7 @@ def tile_cvim_pa_kernel(tc, x, w1, b1, w2, b2, out_0, out_1):
                     item[0]()
                 else:
                     b, k = item
-                    by_scalar = n_out[0] % SCALAR_CASTS == SCALAR_CASTS - 3
+                    by_scalar = n_out[0] in SCALAR_CASTS
+                    by_vector = n_out[0] in VECTOR_COPIES
                     n_out[0] += 1
-                    tile_out(b, k, by_scalar, lambda fn: late.setdefault(s + 1, []).append((fn,)))
+                    tile_out(b, k, by_scalar, by_vector, lambda fn: late.setdefault(s + 1, []).append((fn,)))

@@ -27,7 +27,7 @@ HEAD_WINDOWS = (0,)
 HEAD_ENGINES = ("s", "s", "s")
 IN_LEAD = 8
 ONE_ONE = 1.0019454956054688
-KICK = 14
+KICK = 9
 KICK_HEAD = 4
 MM_LEAD = 3
 OUT_LEAD = 1

@@ -29,7 +29,7 @@ IN_LEAD = 8
 ONE_ONE = 1.0019454956054688
 KICK = 9
 KICK_HEAD = 4
-MM_LEAD = 3
+MM_LEAD = 2
 OUT_LEAD = 1
 SCALAR_CASTS = (5, 13)
 DIAG = (0, 3)

@@ -29,7 +29,7 @@ IN_LEAD = 8
 ONE_ONE = 1.0019454956054688
 KICK = 9
 KICK_HEAD = 4
-MM_LEAD = 2
+MM_LEAD = {512: 1, 256: 2, 128: 2}
 OUT_LEAD = 1
 SCALAR_CASTS = (5, 13)
 DIAG = (0, 3)
@@ -274,7 +274,10 @@ def tile_cvim_pa_kernel(tc, x, w1, b1, w2, b2, out_0, out_1):
             else:
                 cast_later(cast)
 
-        first = -MM_LEAD
+        mm_at = {}
+        for u in range(NU):
+            mm_at.setdefault(u - MM_LEAD[WINDOWS[units[u][0]][2]], []).append(u)
+        first = min(mm_at)
         early = {}
         for i in range(NW):
             if i not in HEAD_WINDOWS:
@@ -289,8 +292,8 @@ def tile_cvim_pa_kernel(tc, x, w1, b1, w2, b2, out_0, out_1):
         for s in range(first, NU + 16):
             for i in early.get(s, []):
                 stage_in(i)
-            if 0 <= s + MM_LEAD < NU:
-                unit_mm(s + MM_LEAD)
+            for u in mm_at.get(s, []):
+                unit_mm(u)
             if 0 <= s + 1 < NU:
                 unit_prev(s + 1)
             if 0 <= s < NU:

@@ -30,6 +30,7 @@ ONE_ONE = 1.0019454956054688
 KICK = 9
 KICK_HEAD = 4
 MM_LEAD = {512: 1, 256: 2, 128: 2}
+QUANT_LAG = 1
 OUT_LEAD = 1
 SCALAR_CASTS = (5, 13)
 DIAG = (0, 3)
@@ -149,8 +150,10 @@ def tile_cvim_pa_kernel(tc, x, w1, b1, w2, b2, out_0, out_1):
                     nc.vector.tensor_copy(out=dst, in_=turned[:, 0:na].rearrange("p a u r -> p a r u"))
                 else:
                     nc.scalar.copy(out=dst, in_=turned[:, 0:na].rearrange("p a u r -> p a r u"))
-            nc.vector.quantize_mx(out=codes[:].bitcast(FP8X4), scales=scales[:], in_=grouped[:])
-            return codes, scales
+            def quantise():
+                nc.vector.quantize_mx(out=codes[:].bitcast(FP8X4), scales=scales[:], in_=grouped[:])
+
+            return codes, scales, quantise
 
         w_mx = {}
         x_mx = {}
@@ -162,7 +165,8 @@ def tile_cvim_pa_kernel(tc, x, w1, b1, w2, b2, out_0, out_1):
                     slots.append(w_raw[item[1]].bitcast(F32))
                 else:
                     slots.append(x_raw[item[1]][:, item[2], :].bitcast(F32))
-            codes, scales = to_mx(slots, "h%d" % q, HEAD_ENGINES[q])
+            codes, scales, quantise = to_mx(slots, "h%d" % q, HEAD_ENGINES[q])
+            quantise()
             for a, item in enumerate(HEAD_STAGES[q]):
                 cols = slice(a * P, (a + 1) * P)
                 if item[0] == "w":
@@ -174,8 +178,9 @@ def tile_cvim_pa_kernel(tc, x, w1, b1, w2, b2, out_0, out_1):
         def stage_in(i):
             n = WINDOWS[i][2]
             xw = x_raw[i][:].bitcast(F32)
-            codes, scales = to_mx([xw[:, a, :] for a in range(n // P)], "x%d" % i, "s")
+            codes, scales, quantise = to_mx([xw[:, a, :] for a in range(n // P)], "x%d" % i, "s")
             x_mx[i] = (codes[:], scales[:])
+            return quantise
 
         units = [(i, j) for i in range(NW) for j in range(ND)]
         NU = len(units)
@@ -291,7 +296,7 @@ def tile_cvim_pa_kernel(tc, x, w1, b1, w2, b2, out_0, out_1):
             kick(KICK_HEAD)
         for s in range(first, NU + 16):
             for i in early.get(s, []):
-                stage_in(i)
+                late.setdefault(s + QUANT_LAG, []).append((stage_in(i),))
             for u in mm_at.get(s, []):
                 unit_mm(u)
             if 0 <= s + 1 < NU:

@@ -52,10 +52,6 @@ def tile_cvim_pa_kernel(tc, x, w1, b1, w2, b2, out_0, out_1):
         w2_b = const.tile([P, ND, KW], BF16, name="w2_b")
         b1_b = const.tile([P, ND], BF16, name="b1_b")
         b2_b = const.tile([P, ND], BF16, name="b2_b")
-        with nc.allow_non_contiguous_dma(reason="one value of a 512-long vector to a partition"):
-            nc.scalar.dma_start(out=w2_b[:], in_=w2.rearrange("(j p) k -> p j k", p=P))
-            nc.scalar.dma_start(out=b1_b[:], in_=b1.rearrange("(j p) -> p j", p=P))
-            nc.scalar.dma_start(out=b2_b[:], in_=b2.rearrange("(j p) -> p j", p=P))
 
         w_view = w1.rearrange("(j p) c -> p j c", p=P)
         w_raw = {}
@@ -76,6 +72,10 @@ def tile_cvim_pa_kernel(tc, x, w1, b1, w2, b2, out_0, out_1):
         load_w(0, 2)
         load_x(0)
         load_w(2, 4)
+        with nc.allow_non_contiguous_dma(reason="one value of a 512-long vector to a partition"):
+            nc.sync.dma_start(out=w2_b[:], in_=w2.rearrange("(j p) k -> p j k", p=P))
+            nc.sync.dma_start(out=b1_b[:], in_=b1.rearrange("(j p) -> p j", p=P))
+            nc.sync.dma_start(out=b2_b[:], in_=b2.rearrange("(j p) -> p j", p=P))
         for i in range(1, NW):
             load_x(i)
 

@@ -29,6 +29,7 @@ IN_LEAD = 8
 ONE_ONE = 1.0019454956054688
 KICK = 9
 KICK_HEAD = 4
+KICK_TAIL = 3
 MM_LEAD = {512: 1, 256: 2, 128: 2}
 QUANT_LAG = 1
 OUT_LEAD = 1
@@ -90,10 +91,10 @@ def tile_cvim_pa_kernel(tc, x, w1, b1, w2, b2, out_0, out_1):
         nc.vector.quantize_mx(out=ones_codes[:].bitcast(FP8X4), scales=ones_scales[:], in_=ones[:])
         idle = psum.tile([P, 512], F32, name="bank")
 
-        def kick(times):
+        def kick(times, bank=idle):
             for r in range(times):
                 nc.tensor.matmul_mx(
-                    out=idle[:, 0:P], lhsT=ones_codes[:].bitcast(FP8X4), lhsT_scale=ones_scales[:],
+                    out=bank[:, 0:P], lhsT=ones_codes[:].bitcast(FP8X4), lhsT_scale=ones_scales[:],
                     rhs=ones_codes[:].bitcast(FP8X4), rhs_scale=ones_scales[:], start=True, stop=True,
                 )
 
@@ -248,6 +249,8 @@ def tile_cvim_pa_kernel(tc, x, w1, b1, w2, b2, out_0, out_1):
 
         def tile_out(b, k, by_scalar, by_vector, cast_later):
             bank = psum.tile([P, 512], F32, name="bank")
+            if b == B - 1 and k >= T // P - 4:
+                kick(KICK_TAIL, bank)
             for j in range(ND):
                 if (b, j) == DIAG:
                     nc.tensor.matmul(out=bank[:, j * P : (j + 1) * P], lhsT=b2_rep[:], rhs=ident[:], is_transpose=True, start=True, stop=False)

@@ -22,6 +22,7 @@ ND = D // P
 WORDS = C // 2
 
 WINDOWS = [(0, 0, 256), (0, 256, 256), (0, 512, 512), (1, 0, 512), (1, 512, 256), (1, 768, 128), (1, 896, 128)]
+GROUP = {6: 5}
 HEAD_STAGES = [[("w", 0), ("w", 1)], [("x", 0, 0), ("x", 0, 1)], [("w", 2), ("w", 3)]]
 HEAD_WINDOWS = (0,)
 HEAD_ENGINES = ("s", "s", "s")
@@ -36,6 +37,7 @@ OUT_LEAD = 1
 SCALAR_CASTS = (5, 13)
 DIAG = (0, 3)
 VECTOR_COPIES = ()
+LAST_PARTS = ((0, 2), (2, 4))
 
 
 def tile_cvim_pa_kernel(tc, x, w1, b1, w2, b2, out_0, out_1):
@@ -64,8 +66,12 @@ def tile_cvim_pa_kernel(tc, x, w1, b1, w2, b2, out_0, out_1):
             for j in range(j0, j1):
                 w_raw[j] = wr[:, j - j0, :]
 
+        def span(i):
+            return WINDOWS[i][2] + sum([WINDOWS[f][2] for f in GROUP if GROUP[f] == i])
+
         def load_x(i):
             b, t0, n = WINDOWS[i]
+            n = span(i)
             xr = const.tile([P, n // P, C], BF16, name="x_raw%d" % i)
             nc.sync.dma_start(out=xr[:], in_=x[b, t0 : t0 + n, :].rearrange("(n p) c -> p n c", p=P))
             x_raw[i] = xr
@@ -78,7 +84,8 @@ def tile_cvim_pa_kernel(tc, x, w1, b1, w2, b2, out_0, out_1):
             nc.sync.dma_start(out=b1_b[:], in_=b1.rearrange("(j p) -> p j", p=P))
             nc.sync.dma_start(out=b2_b[:], in_=b2.rearrange("(j p) -> p j", p=P))
         for i in range(1, NW):
-            load_x(i)
+            if i not in GROUP:
+                load_x(i)
 
         warm = const.tile([P, 1], F32, name="warm")
         nc.vector.memset(warm[:], 0.0)
@@ -177,7 +184,7 @@ def tile_cvim_pa_kernel(tc, x, w1, b1, w2, b2, out_0, out_1):
                     x_mx[item[1]] = (codes[:, a * P : a * P + n], scales[:, a * P : a * P + n])
 
         def stage_in(i):
-            n = WINDOWS[i][2]
+            n = span(i)
             xw = x_raw[i][:].bitcast(F32)
             codes, scales, quantise = to_mx([xw[:, a, :] for a in range(n // P)], "x%d" % i, "s")
             x_mx[i] = (codes[:], scales[:])
@@ -189,7 +196,7 @@ def tile_cvim_pa_kernel(tc, x, w1, b1, w2, b2, out_0, out_1):
 
         def unit_mm(s):
             i, j = units[s]
-            n = WINDOWS[i][2]
+            n = span(i)
             x_codes, x_scales = x_mx[i]
             w_codes, w_scales = w_mx[j]
             bank = psum.tile([P, 512], F32, name="bank")
@@ -202,7 +209,12 @@ def tile_cvim_pa_kernel(tc, x, w1, b1, w2, b2, out_0, out_1):
                 start=True,
                 stop=True,
             )
-            accs[s] = bank
+            accs[s] = bank[:, 0 : WINDOWS[i][2] + (1 if n > WINDOWS[i][2] else 0)]
+            off = WINDOWS[i][2]
+            for f in sorted(GROUP):
+                if GROUP[f] == i:
+                    accs[s + ND * (f - i)] = bank[:, off : off + WINDOWS[f][2]]
+                    off += WINDOWS[f][2]
 
         def unit_prev(s):
             i, j = units[s]
@@ -236,10 +248,11 @@ def tile_cvim_pa_kernel(tc, x, w1, b1, w2, b2, out_0, out_1):
             if (b, j) == DIAG:
                 return
             yj = y[b][:, j, :]
-            lo = 1 if t0 == 0 else 0
+            lo = 1 if t0 == 0 or i in GROUP else 0
+            hi = n + 1 if i + 1 in GROUP else n
             nc.vector.scalar_tensor_tensor(
-                out=yj[:, t0 + lo - 1 : t0 + n - 1], in0=accs[s][:, lo:n], scalar=taps[:, j, 2:3],
-                in1=yj[:, t0 + lo - 1 : t0 + n - 1], op0=ALU.mult, op1=ALU.add,
+                out=yj[:, t0 + lo - 1 : t0 + hi - 1], in0=accs[s][:, lo:hi], scalar=taps[:, j, 2:3],
+                in1=yj[:, t0 + lo - 1 : t0 + hi - 1], op0=ALU.mult, op1=ALU.add,
             )
 
         def last_column(b):
@@ -248,47 +261,54 @@ def tile_cvim_pa_kernel(tc, x, w1, b1, w2, b2, out_0, out_1):
             nc.vector.tensor_tensor(out=col, in0=col, in1=edge2[:, 0:nj].unsqueeze(2), op=ALU.subtract)
 
         def tile_out(b, k, by_scalar, by_vector, cast_later):
-            bank = psum.tile([P, 512], F32, name="bank")
-            if b == B - 1 and k >= T // P - 4:
-                kick(KICK_TAIL, bank)
-            for j in range(ND):
-                if (b, j) == DIAG:
-                    nc.tensor.matmul(out=bank[:, j * P : (j + 1) * P], lhsT=b2_rep[:], rhs=ident[:], is_transpose=True, start=True, stop=False)
-                    for r in range(KW):
-                        nc.tensor.matmul(
-                            out=bank[:, j * P : (j + 1) * P], lhsT=hpad[:, k * P + r : (k + 1) * P + r], rhs=diag[:, r, :],
-                            start=False, stop=(r == KW - 1),
-                        )
-                else:
-                    nc.tensor.transpose(out=bank[:, j * P : (j + 1) * P], in_=y[b][:, j, k * P : (k + 1) * P], identity=ident[:])
             rows = slice(b * T + k * P, b * T + (k + 1) * P)
             r32 = res.tile([P, D], F32, name="r32")
             r8 = res.tile([P, D], FP8, name="r8")
-            if by_vector:
-                nc.vector.tensor_copy(out=r32[:], in_=bank[:])
-            else:
-                nc.scalar.copy(out=r32[:], in_=bank[:])
-            nc.sync.dma_start(out=o0[rows, :], in_=r32[:])
-
-            def cast():
-                if by_scalar:
-                    nc.scalar.activation(out=r8[:], in_=bank[:], func=ACT.Copy, scale=Y_SCALE, saturate=False)
+            last = b == B - 1 and k == T // P - 1
+            parts = LAST_PARTS if last else ((0, ND),)
+            for j0, j1 in parts:
+                bank = psum.tile([P, 512], F32, name="bank")
+                if b == B - 1 and k >= T // P - 4 and j0 == 0:
+                    kick(KICK_TAIL, bank)
+                for j in range(j0, j1):
+                    there = bank[:, (j - j0) * P : (j - j0 + 1) * P]
+                    if (b, j) == DIAG:
+                        nc.tensor.matmul(out=there, lhsT=b2_rep[:], rhs=ident[:], is_transpose=True, start=True, stop=False)
+                        for r in range(KW):
+                            nc.tensor.matmul(
+                                out=there, lhsT=hpad[:, k * P + r : (k + 1) * P + r], rhs=diag[:, r, :],
+                                start=False, stop=(r == KW - 1),
+                            )
+                    else:
+                        nc.tensor.transpose(out=there, in_=y[b][:, j, k * P : (k + 1) * P], identity=ident[:])
+                cols = slice(j0 * P, j1 * P)
+                turned = bank[:, 0 : (j1 - j0) * P]
+                if by_vector:
+                    nc.vector.tensor_copy(out=r32[:, cols], in_=turned)
                 else:
-                    nc.vector.tensor_scalar(out=r8[:], in0=r32[:], scalar1=Y_SCALE, scalar2=None, op0=ALU.mult, saturate=False)
-                nc.sync.dma_start(out=o1[rows, :], in_=r8[:].bitcast(U8))
+                    nc.scalar.copy(out=r32[:, cols], in_=turned)
+                nc.sync.dma_start(out=o0[rows, cols], in_=r32[:, cols])
 
-            if by_scalar:
-                cast()
-            else:
-                cast_later(cast)
+                def cast(cols=cols, turned=turned):
+                    if by_scalar:
+                        nc.scalar.activation(out=r8[:, cols], in_=turned, func=ACT.Copy, scale=Y_SCALE, saturate=False)
+                    else:
+                        nc.vector.tensor_scalar(out=r8[:, cols], in0=r32[:, cols], scalar1=Y_SCALE, scalar2=None, op0=ALU.mult, saturate=False)
+                    nc.sync.dma_start(out=o1[rows, cols], in_=r8[:, cols].bitcast(U8))
+
+                if by_scalar:
+                    cast()
+                else:
+                    cast_later(cast)
 
         mm_at = {}
         for u in range(NU):
-            mm_at.setdefault(u - MM_LEAD[WINDOWS[units[u][0]][2]], []).append(u)
+            if units[u][0] not in GROUP:
+                mm_at.setdefault(u - MM_LEAD[span(units[u][0])], []).append(u)
         first = min(mm_at)
         early = {}
         for i in range(NW):
-            if i not in HEAD_WINDOWS:
+            if i not in HEAD_WINDOWS and i not in GROUP:
                 early.setdefault(max(first, ND * i - IN_LEAD), []).append(i)
         late = {}
         done = {0: 0, 1: 0}
@@ -325,7 +345,7 @@ def tile_cvim_pa_kernel(tc, x, w1, b1, w2, b2, out_0, out_1):
                 else:
                     unit_next(s - 1)
                 if j == ND - 1:
-                    ready = T // P if t0 + n == T else (t0 + n - 1) // P
+                    ready = T // P if t0 + n == T else ((t0 + n) // P if i + 1 in GROUP else (t0 + n - 1) // P)
                     for r, k in enumerate(range(done[b], ready)):
                         late.setdefault(s + OUT_LEAD + r, []).append((b, k))
                     done[b] = ready

@@ -287,14 +287,16 @@ def tile_cvim_pa_kernel(tc, x, w1, b1, w2, b2, out_0, out_1):
                     nc.vector.tensor_copy(out=r32[:, cols], in_=turned)
                 else:
                     nc.scalar.copy(out=r32[:, cols], in_=turned)
-                nc.sync.dma_start(out=o0[rows, cols], in_=r32[:, cols])
+                if j1 == ND:
+                    nc.sync.dma_start(out=o0[rows, :], in_=r32[:])
 
-                def cast(cols=cols, turned=turned):
+                def cast(cols=cols, turned=turned, j1=j1):
                     if by_scalar:
                         nc.scalar.activation(out=r8[:, cols], in_=turned, func=ACT.Copy, scale=Y_SCALE, saturate=False)
                     else:
                         nc.vector.tensor_scalar(out=r8[:, cols], in0=r32[:, cols], scalar1=Y_SCALE, scalar2=None, op0=ALU.mult, saturate=False)
-                    nc.sync.dma_start(out=o1[rows, cols], in_=r8[:, cols].bitcast(U8))
+                    if j1 == ND:
+                        nc.sync.dma_start(out=o1[rows, :], in_=r8[:].bitcast(U8))
 
                 if by_scalar:
                     cast()

@@ -37,6 +37,7 @@ OUT_LEAD = 1
 SCALAR_CASTS = (5, 13)
 DIAG = (0, 3)
 VECTOR_COPIES = ()
+BYTES_GROUPS = ((11, 12), (13, 14))
 LAST_PARTS = ((0, 2), (2, 4))
 
 
@@ -260,10 +261,18 @@ def tile_cvim_pa_kernel(tc, x, w1, b1, w2, b2, out_0, out_1):
             col = y[b][:, 0:nj, T - 1 : T]
             nc.vector.tensor_tensor(out=col, in0=col, in1=edge2[:, 0:nj].unsqueeze(2), op=ALU.subtract)
 
-        def tile_out(b, k, by_scalar, by_vector, cast_later):
+        shared = {}
+
+        def tile_out(b, k, n, by_scalar, by_vector, cast_later):
             rows = slice(b * T + k * P, b * T + (k + 1) * P)
             r32 = res.tile([P, D], F32, name="r32")
-            r8 = res.tile([P, D], FP8, name="r8")
+            group = ([g for g in BYTES_GROUPS if n in g] + [(n,)])[0]
+            q = group.index(n)
+            if q == 0:
+                r8_new = res.tile([P, len(group), D], FP8, name="r8")
+                shared["r8"] = r8_new
+            r8g = shared["r8"]
+            group_rows = slice(b * T + (k - q) * P, b * T + (k - q + len(group)) * P)
             last = b == B - 1 and k == T // P - 1
             parts = LAST_PARTS if last else ((0, ND),)
             for j0, j1 in parts:
@@ -289,14 +298,15 @@ def tile_cvim_pa_kernel(tc, x, w1, b1, w2, b2, out_0, out_1):
                     nc.scalar.copy(out=r32[:, cols], in_=turned)
                 if j1 == ND:
                     nc.sync.dma_start(out=o0[rows, :], in_=r32[:])
+                whole = q == len(group) - 1 and j1 == ND
 
-                def cast(cols=cols, turned=turned, j1=j1):
+                def cast(cols=cols, turned=turned, whole=whole):
                     if by_scalar:
-                        nc.scalar.activation(out=r8[:, cols], in_=turned, func=ACT.Copy, scale=Y_SCALE, saturate=False)
+                        nc.scalar.activation(out=r8g[:, q, cols], in_=turned, func=ACT.Copy, scale=Y_SCALE, saturate=False)
                     else:
-                        nc.vector.tensor_scalar(out=r8[:, cols], in0=r32[:, cols], scalar1=Y_SCALE, scalar2=None, op0=ALU.mult, saturate=False)
-                    if j1 == ND:
-                        nc.sync.dma_start(out=o1[rows, :], in_=r8[:].bitcast(U8))
+                        nc.vector.tensor_scalar(out=r8g[:, q, cols], in0=r32[:, cols], scalar1=Y_SCALE, scalar2=None, op0=ALU.mult, saturate=False)
+                    if whole:
+                        nc.sync.dma_start(out=o1[group_rows, :].rearrange("(q p) d -> p q d", p=P), in_=r8g[:].bitcast(U8))
 
                 if by_scalar:
                     cast()
@@ -359,4 +369,4 @@ def tile_cvim_pa_kernel(tc, x, w1, b1, w2, b2, out_0, out_1):
                     by_scalar = n_out[0] in SCALAR_CASTS
                     by_vector = n_out[0] in VECTOR_COPIES
                     n_out[0] += 1
-                    tile_out(b, k, by_scalar, by_vector, lambda fn: late.setdefault(s + 1, []).append((fn,)))
+                    tile_out(b, k, n_out[0] - 1, by_scalar, by_vector, lambda fn: late.setdefault(s + 1, []).append((fn,)))

@@ -22,6 +22,7 @@ ND = D // P
 WORDS = C // 2
 
 WINDOWS = [(0, 0, 256), (0, 256, 256), (0, 512, 512), (1, 0, 512), (1, 512, 256), (1, 768, 128), (1, 896, 128)]
+PAIRED = (0, 1, 4)
 GROUP = {6: 5}
 HEAD_STAGES = [[("w", 0), ("w", 1)], [("x", 0, 0), ("x", 0, 1)], [("w", 2), ("w", 3)]]
 HEAD_WINDOWS = (0,)
@@ -199,18 +200,19 @@ def tile_cvim_pa_kernel(tc, x, w1, b1, w2, b2, out_0, out_1):
             i, j = units[s]
             n = span(i)
             x_codes, x_scales = x_mx[i]
-            w_codes, w_scales = w_mx[j]
             bank = psum.tile([P, 512], F32, name="bank")
-            nc.tensor.matmul_mx(
-                out=bank[:, 0:n],
-                lhsT=w_codes.bitcast(FP8X4),
-                lhsT_scale=w_scales,
-                rhs=x_codes.bitcast(FP8X4),
-                rhs_scale=x_scales,
-                start=True,
-                stop=True,
-            )
-            accs[s] = bank[:, 0 : WINDOWS[i][2] + (1 if n > WINDOWS[i][2] else 0)]
+            for e in range(2 if i in PAIRED else 1):
+                w_codes, w_scales = w_mx[j + e]
+                nc.tensor.matmul_mx(
+                    out=bank[:, e * n : (e + 1) * n],
+                    lhsT=w_codes.bitcast(FP8X4),
+                    lhsT_scale=w_scales,
+                    rhs=x_codes.bitcast(FP8X4),
+                    rhs_scale=x_scales,
+                    start=True,
+                    stop=True,
+                )
+                accs[s + e] = bank[:, e * n : e * n + WINDOWS[i][2] + (1 if n > WINDOWS[i][2] else 0)]
             off = WINDOWS[i][2]
             for f in sorted(GROUP):
                 if GROUP[f] == i:
@@ -314,9 +316,16 @@ def tile_cvim_pa_kernel(tc, x, w1, b1, w2, b2, out_0, out_1):
                     cast_later(cast)
 
         mm_at = {}
+        prev_at = {}
         for u in range(NU):
-            if units[u][0] not in GROUP:
-                mm_at.setdefault(u - MM_LEAD[span(units[u][0])], []).append(u)
+            if units[u][0] in PAIRED:
+                if units[u][1] % 2 == 0:
+                    mm_at.setdefault(u - 3, []).append(u)
+                prev_at.setdefault(u - 2, []).append(u)
+            else:
+                if units[u][0] not in GROUP:
+                    mm_at.setdefault(u - MM_LEAD[span(units[u][0])], []).append(u)
+                prev_at.setdefault(u - 1, []).append(u)
         first = min(mm_at)
         early = {}
         for i in range(NW):
@@ -334,8 +343,8 @@ def tile_cvim_pa_kernel(tc, x, w1, b1, w2, b2, out_0, out_1):
                 late.setdefault(s + QUANT_LAG, []).append((stage_in(i),))
             for u in mm_at.get(s, []):
                 unit_mm(u)
-            if 0 <= s + 1 < NU:
-                unit_prev(s + 1)
+            for u in prev_at.get(s, []):
+                unit_prev(u)
             if 0 <= s < NU:
                 i, j = units[s]
                 b, t0, n = WINDOWS[i]

@@ -31,7 +31,7 @@ IN_LEAD = 8
 ONE_ONE = 1.0019454956054688
 KICK = 9
 KICK_HEAD = 4
-KICK_TAIL = 3
+KICK_TAIL = 0
 MM_LEAD = {512: 1, 256: 2, 128: 2}
 QUANT_LAG = 1
 OUT_LEAD = 1

@@ -36,7 +36,7 @@ MM_LEAD = {512: 1, 256: 2, 128: 2}
 QUANT_LAG = 1
 OUT_LEAD = 1
 SCALAR_CASTS = (5, 13)
-DIAG = (0, 3)
+DIAG_UNITS = ((1, 3), (2, 3))
 VECTOR_COPIES = ()
 BYTES_GROUPS = ((11, 12), (13, 14))
 LAST_PARTS = ((0, 2), (2, 4))
@@ -131,16 +131,28 @@ def tile_cvim_pa_kernel(tc, x, w1, b1, w2, b2, out_0, out_1):
             nc.vector.tensor_copy(out=yb[:, :, 0:1], in_=beta_first[:].unsqueeze(2))
             y.append(yb)
 
-        hpad = const.tile([P, T + 2], F32, name="hpad")
-        nc.vector.memset(hpad[:, 0:1], 0.0)
-        nc.vector.memset(hpad[:, T + 1 : T + 2], 0.0)
+        def beside(i, step):
+            e = i + step
+            return e if 0 <= e < NW and WINDOWS[e][0] == WINDOWS[i][0] else None
+
+        hpad = {}
+        for b, j in sorted(set([(WINDOWS[i][0], j) for i, j in DIAG_UNITS])):
+            hp = const.tile([P, T + 2], F32, name="hpad%d_%d" % (b, j))
+            nc.vector.memset(hp[:, 0:1], 0.0)
+            nc.vector.memset(hp[:, T + 1 : T + 2], 0.0)
+            hpad[(b, j)] = hp
         b1_f = const.tile([P, ND], F32, name="b1_f")
         nc.vector.tensor_copy(out=b1_f[:], in_=b1_b[:])
-        diag = const.tile([P, KW, P], F32, name="diag")
-        for r in range(KW):
-            nc.vector.tensor_scalar(out=diag[:, r, :], in0=ident[:], scalar1=taps[:, DIAG[1], r : r + 1], scalar2=None, op0=ALU.mult)
-        b2_rep = const.tile([P, P], F32, name="b2_rep")
-        nc.vector.tensor_copy(out=b2_rep[:], in_=b2_b[:, DIAG[1] : DIAG[1] + 1].to_broadcast([P, P]))
+        diag = {}
+        b2_rep = {}
+        for j in sorted(set([u[1] for u in DIAG_UNITS])):
+            dg = const.tile([P, KW, P], F32, name="diag%d" % j)
+            for r in range(KW):
+                nc.vector.tensor_scalar(out=dg[:, r, :], in0=ident[:], scalar1=taps[:, j, r : r + 1], scalar2=None, op0=ALU.mult)
+            br = const.tile([P, P], F32, name="b2_rep%d" % j)
+            nc.vector.tensor_copy(out=br[:], in_=b2_b[:, j : j + 1].to_broadcast([P, P]))
+            diag[j] = dg
+            b2_rep[j] = br
 
         def to_mx(slots, name, engine):
             nt = len(slots)
@@ -222,13 +234,30 @@ def tile_cvim_pa_kernel(tc, x, w1, b1, w2, b2, out_0, out_1):
         def unit_prev(s):
             i, j = units[s]
             b, t0, n = WINDOWS[i]
-            if (b, j) == DIAG:
+            before, after = beside(i, -1), beside(i, 1)
+            if (i, j) in DIAG_UNITS:
                 nc.scalar.activation(
-                    out=hpad[:, 1 + t0 : 1 + t0 + n], in_=accs[s][:, 0:n], func=ACT.Identity,
+                    out=hpad[(b, j)][:, 1 + t0 : 1 + t0 + n], in_=accs[s][:, 0:n], func=ACT.Identity,
                     bias=b1_f[:, j : j + 1], scale=1.0,
                 )
+                if after is not None and (after, j) not in DIAG_UNITS:
+                    nc.scalar.activation(
+                        out=y[b][:, j, t0 + n : t0 + n + 1], in_=accs[s][:, n - 1 : n], func=ACT.Identity,
+                        bias=beta[:, j : j + 1], scale=taps[:, j, 0:1],
+                    )
                 return
+            if before is not None and (before, j) in DIAG_UNITS:
+                nc.scalar.activation(
+                    out=hpad[(b, j)][:, 1 + t0 : 2 + t0], in_=accs[s][:, 0:1], func=ACT.Identity,
+                    bias=b1_f[:, j : j + 1], scale=1.0,
+                )
             m = n if t0 + n < T else n - 1
+            if after is not None and (after, j) in DIAG_UNITS:
+                nc.scalar.activation(
+                    out=hpad[(b, j)][:, t0 + n : t0 + n + 1], in_=accs[s][:, n - 1 : n], func=ACT.Identity,
+                    bias=b1_f[:, j : j + 1], scale=1.0,
+                )
+                m = n - 1
             nc.scalar.activation(
                 out=y[b][:, j, t0 + 1 : t0 + 1 + m], in_=accs[s][:, 0:m], func=ACT.Identity,
                 bias=beta[:, j : j + 1], scale=taps[:, j, 0:1],
@@ -237,7 +266,7 @@ def tile_cvim_pa_kernel(tc, x, w1, b1, w2, b2, out_0, out_1):
         def unit_mid(s):
             i, j = units[s]
             b, t0, n = WINDOWS[i]
-            if (b, j) == DIAG:
+            if (i, j) in DIAG_UNITS:
                 return
             yj = y[b][:, j, :]
             nc.vector.scalar_tensor_tensor(
@@ -248,18 +277,21 @@ def tile_cvim_pa_kernel(tc, x, w1, b1, w2, b2, out_0, out_1):
         def unit_next(s):
             i, j = units[s]
             b, t0, n = WINDOWS[i]
-            if (b, j) == DIAG:
-                return
+            before = beside(i, -1)
             yj = y[b][:, j, :]
-            lo = 1 if t0 == 0 or i in GROUP else 0
+            lo = 1 if t0 == 0 or i in GROUP or (before, j) in DIAG_UNITS else 0
             hi = n + 1 if i + 1 in GROUP else n
+            if (i, j) in DIAG_UNITS:
+                if before is None or (before, j) in DIAG_UNITS:
+                    return
+                hi = 1
             nc.vector.scalar_tensor_tensor(
                 out=yj[:, t0 + lo - 1 : t0 + hi - 1], in0=accs[s][:, lo:hi], scalar=taps[:, j, 2:3],
                 in1=yj[:, t0 + lo - 1 : t0 + hi - 1], op0=ALU.mult, op1=ALU.add,
             )
 
         def last_column(b):
-            nj = DIAG[1] if b == DIAG[0] else ND
+            nj = min([ND] + [j for i, j in DIAG_UNITS if WINDOWS[i][0] == b and WINDOWS[i][1] + WINDOWS[i][2] == T])
             col = y[b][:, 0:nj, T - 1 : T]
             nc.vector.tensor_tensor(out=col, in0=col, in1=edge2[:, 0:nj].unsqueeze(2), op=ALU.subtract)
 
@@ -283,11 +315,13 @@ def tile_cvim_pa_kernel(tc, x, w1, b1, w2, b2, out_0, out_1):
                     kick(KICK_TAIL, bank)
                 for j in range(j0, j1):
                     there = bank[:, (j - j0) * P : (j - j0 + 1) * P]
-                    if (b, j) == DIAG:
-                        nc.tensor.matmul(out=there, lhsT=b2_rep[:], rhs=ident[:], is_transpose=True, start=True, stop=False)
+                    home = [i for i in range(NW) if WINDOWS[i][0] == b and WINDOWS[i][1] <= k * P < WINDOWS[i][1] + WINDOWS[i][2]][0]
+                    if (home, j) in DIAG_UNITS:
+                        c0 = k * P
+                        nc.tensor.matmul(out=there, lhsT=b2_rep[j][:], rhs=ident[:], is_transpose=True, start=True, stop=False)
                         for r in range(KW):
                             nc.tensor.matmul(
-                                out=there, lhsT=hpad[:, k * P + r : (k + 1) * P + r], rhs=diag[:, r, :],
+                                out=there, lhsT=hpad[(b, j)][:, c0 + r : c0 + P + r], rhs=diag[j][:, r, :],
                                 start=False, stop=(r == KW - 1),
                             )
                     else:

@@ -58,13 +58,13 @@ def tile_cvim_pa_kernel(tc, x, w1, b1, w2, b2, out_0, out_1):
         b1_b = const.tile([P, ND], BF16, name="b1_b")
         b2_b = const.tile([P, ND], BF16, name="b2_b")
 
-        w_view = w1.rearrange("(j p) c -> p j c", p=P)
+        w_view = w1.rearrange("(h p l) c -> h p l c", h=2, l=2)
         w_raw = {}
         x_raw = {}
 
         def load_w(j0, j1):
             wr = const.tile([P, j1 - j0, C], BF16, name="w_raw%d" % j0)
-            nc.sync.dma_start(out=wr[:], in_=w_view[:, j0:j1, :])
+            nc.sync.dma_start(out=wr[:], in_=w_view[j0 // 2])
             for j in range(j0, j1):
                 w_raw[j] = wr[:, j - j0, :]
 
@@ -82,9 +82,9 @@ def tile_cvim_pa_kernel(tc, x, w1, b1, w2, b2, out_0, out_1):
         load_x(0)
         load_w(2, 4)
         with nc.allow_non_contiguous_dma(reason="one value of a 512-long vector to a partition"):
-            nc.sync.dma_start(out=w2_b[:], in_=w2.rearrange("(j p) k -> p j k", p=P))
-            nc.sync.dma_start(out=b1_b[:], in_=b1.rearrange("(j p) -> p j", p=P))
-            nc.sync.dma_start(out=b2_b[:], in_=b2.rearrange("(j p) -> p j", p=P))
+            nc.sync.dma_start(out=w2_b[:].rearrange("p (h l) k -> p h (l k)", h=2), in_=w2.rearrange("(h p l) k -> p h (l k)", h=2, l=2))
+            nc.sync.dma_start(out=b1_b[:].rearrange("p (h l) -> p h l", h=2), in_=b1.rearrange("(h p l) -> p h l", h=2, l=2))
+            nc.sync.dma_start(out=b2_b[:].rearrange("p (h l) -> p h l", h=2), in_=b2.rearrange("(h p l) -> p h l", h=2, l=2))
         for i in range(1, NW):
             if i not in GROUP:
                 load_x(i)
@@ -328,17 +328,17 @@ def tile_cvim_pa_kernel(tc, x, w1, b1, w2, b2, out_0, out_1):
                         nc.tensor.transpose(out=there, in_=y[b][:, j, k * P : (k + 1) * P], identity=ident[:])
                 cols = slice(j0 * P, j1 * P)
                 turned = bank[:, 0 : (j1 - j0) * P]
-                if by_vector:
-                    nc.vector.tensor_copy(out=r32[:, cols], in_=turned)
-                else:
-                    nc.scalar.copy(out=r32[:, cols], in_=turned)
+                nc.scalar.copy(
+                    out=r32[:, cols].rearrange("t (h p l) -> t h p l", p=P, l=2),
+                    in_=turned.rearrange("t (h l p) -> t h p l", p=P, l=2),
+                )
                 if j1 == ND:
                     nc.sync.dma_start(out=o0[rows, :], in_=r32[:])
                 whole = q == len(group) - 1 and j1 == ND
 
                 def cast(cols=cols, turned=turned, whole=whole):
                     if by_scalar:
-                        nc.scalar.activation(out=r8g[:, q, cols], in_=turned, func=ACT.Copy, scale=Y_SCALE, saturate=False)
+                        nc.scalar.activation(out=r8g[:, q, cols], in_=r32[:, cols], func=ACT.Copy, scale=Y_SCALE, saturate=False)
                     else:
                         nc.vector.tensor_scalar(out=r8g[:, q, cols], in0=r32[:, cols], scalar1=Y_SCALE, scalar2=None, op0=ALU.mult, saturate=False)
                     if whole:

@@ -22,7 +22,7 @@ ND = D // P
 WORDS = C // 2
 
 WINDOWS = [(0, 0, 256), (0, 256, 256), (0, 512, 512), (1, 0, 512), (1, 512, 256), (1, 768, 128), (1, 896, 128)]
-PAIRED = (0, 1, 4)
+PAIRED = (1, 4)
 GROUP = {6: 5}
 HEAD_STAGES = [[("w", 0), ("w", 1)], [("x", 0, 0), ("x", 0, 1)], [("w", 2), ("w", 3)]]
 HEAD_WINDOWS = (0,)
@@ -314,7 +314,10 @@ def tile_cvim_pa_kernel(tc, x, w1, b1, w2, b2, out_0, out_1):
                 if b == B - 1 and k >= T // P - 4 and j0 == 0:
                     kick(KICK_TAIL, bank)
                 for j in range(j0, j1):
-                    there = bank[:, (j - j0) * P : (j - j0 + 1) * P]
+                    if by_scalar:
+                        there = bank[:, 2 * P * (j // 2) + j % 2 : 2 * P * (j // 2 + 1) : 2]
+                    else:
+                        there = bank[:, (j - j0) * P : (j - j0 + 1) * P]
                     home = [i for i in range(NW) if WINDOWS[i][0] == b and WINDOWS[i][1] <= k * P < WINDOWS[i][1] + WINDOWS[i][2]][0]
                     if (home, j) in DIAG_UNITS:
                         c0 = k * P
@@ -328,17 +331,20 @@ def tile_cvim_pa_kernel(tc, x, w1, b1, w2, b2, out_0, out_1):
                         nc.tensor.transpose(out=there, in_=y[b][:, j, k * P : (k + 1) * P], identity=ident[:])
                 cols = slice(j0 * P, j1 * P)
                 turned = bank[:, 0 : (j1 - j0) * P]
-                nc.scalar.copy(
-                    out=r32[:, cols].rearrange("t (h p l) -> t h p l", p=P, l=2),
-                    in_=turned.rearrange("t (h l p) -> t h p l", p=P, l=2),
-                )
+                if by_scalar:
+                    nc.scalar.copy(out=r32[:, cols], in_=turned)
+                else:
+                    nc.scalar.copy(
+                        out=r32[:, cols].rearrange("t (h p l) -> t h p l", p=P, l=2),
+                        in_=turned.rearrange("t (h l p) -> t h p l", p=P, l=2),
+                    )
                 if j1 == ND:
                     nc.sync.dma_start(out=o0[rows, :], in_=r32[:])
                 whole = q == len(group) - 1 and j1 == ND
 
                 def cast(cols=cols, turned=turned, whole=whole):
                     if by_scalar:
-                        nc.scalar.activation(out=r8g[:, q, cols], in_=r32[:, cols], func=ACT.Copy, scale=Y_SCALE, saturate=False)
+                        nc.scalar.activation(out=r8g[:, q, cols], in_=turned, func=ACT.Copy, scale=Y_SCALE, saturate=False)
                     else:
                         nc.vector.tensor_scalar(out=r8g[:, q, cols], in0=r32[:, cols], scalar1=Y_SCALE, scalar2=None, op0=ALU.mult, saturate=False)
                     if whole:

@@ -22,7 +22,7 @@ ND = D // P
 WORDS = C // 2
 
 WINDOWS = [(0, 0, 256), (0, 256, 256), (0, 512, 512), (1, 0, 512), (1, 512, 256), (1, 768, 128), (1, 896, 128)]
-PAIRED = (1, 4)
+PAIRED = (0, 1, 4)
 GROUP = {6: 5}
 HEAD_STAGES = [[("w", 0), ("w", 1)], [("x", 0, 0), ("x", 0, 1)], [("w", 2), ("w", 3)]]
 HEAD_WINDOWS = (0,)

@@ -377,7 +377,8 @@ def tile_cvim_pa_kernel(tc, x, w1, b1, w2, b2, out_0, out_1):
 
         for q in range(len(HEAD_STAGES)):
             stage_head(q)
-            kick(KICK_HEAD)
+            if q < len(HEAD_STAGES) - 1:
+                kick(KICK_HEAD)
         for s in range(first, NU + 16):
             for i in early.get(s, []):
                 late.setdefault(s + QUANT_LAG, []).append((stage_in(i),))

@@ -80,11 +80,11 @@ def tile_cvim_pa_kernel(tc, x, w1, b1, w2, b2, out_0, out_1):
 
         load_w(0, 2)
         load_x(0)
-        load_w(2, 4)
         with nc.allow_non_contiguous_dma(reason="one value of a 512-long vector to a partition"):
             nc.sync.dma_start(out=w2_b[:].rearrange("p (h l) k -> p h (l k)", h=2), in_=w2.rearrange("(h p l) k -> p h (l k)", h=2, l=2))
             nc.sync.dma_start(out=b1_b[:].rearrange("p (h l) -> p h l", h=2), in_=b1.rearrange("(h p l) -> p h l", h=2, l=2))
             nc.sync.dma_start(out=b2_b[:].rearrange("p (h l) -> p h l", h=2), in_=b2.rearrange("(h p l) -> p h l", h=2, l=2))
+        load_w(2, 4)
         for i in range(1, NW):
             if i not in GROUP:
                 load_x(i)

@@ -23,6 +23,7 @@ WORDS = C // 2
 
 WINDOWS = [(0, 0, 256), (0, 256, 256), (0, 512, 512), (1, 0, 512), (1, 512, 256), (1, 768, 128), (1, 896, 128)]
 PAIRED = (0, 1, 4)
+JOINED_LOADS = {3: (4, 5)}
 GROUP = {6: 5}
 HEAD_STAGES = [[("w", 0), ("w", 1)], [("x", 0, 0), ("x", 0, 1)], [("w", 2), ("w", 3)]]
 HEAD_WINDOWS = (0,)
@@ -73,10 +74,14 @@ def tile_cvim_pa_kernel(tc, x, w1, b1, w2, b2, out_0, out_1):
 
         def load_x(i):
             b, t0, n = WINDOWS[i]
-            n = span(i)
+            members = [i] + [f for f in JOINED_LOADS.get(i, ())]
+            n = sum([span(f) for f in members])
             xr = const.tile([P, n // P, C], BF16, name="x_raw%d" % i)
             nc.sync.dma_start(out=xr[:], in_=x[b, t0 : t0 + n, :].rearrange("(n p) c -> p n c", p=P))
-            x_raw[i] = xr
+            slot = 0
+            for f in members:
+                x_raw[f] = xr[:, slot : slot + span(f) // P, :]
+                slot += span(f) // P
 
         load_w(0, 2)
         load_x(0)
@@ -86,7 +91,7 @@ def tile_cvim_pa_kernel(tc, x, w1, b1, w2, b2, out_0, out_1):
             nc.sync.dma_start(out=b2_b[:].rearrange("p (h l) -> p h l", h=2), in_=b2.rearrange("(h p l) -> p h l", h=2, l=2))
         load_w(2, 4)
         for i in range(1, NW):
-            if i not in GROUP:
+            if i not in GROUP and not any([i in JOINED_LOADS[f] for f in JOINED_LOADS]):
                 load_x(i)
 
         warm = const.tile([P, 1], F32, name="warm")

@@ -39,7 +39,7 @@ OUT_LEAD = 1
 SCALAR_CASTS = (5, 13)
 DIAG_UNITS = ((1, 3), (2, 3))
 VECTOR_COPIES = ()
-BYTES_GROUPS = ((11, 12), (13, 14))
+BYTES_GROUPS = ((0, 1, 2), (3, 4, 5, 6), (8, 9, 10), (11, 12), (13, 14))
 LAST_PARTS = ((0, 2), (2, 4))
 
 

@@ -28,7 +28,7 @@ GROUP = {6: 5}
 HEAD_STAGES = [[("w", 0), ("w", 1)], [("x", 0, 0), ("x", 0, 1)], [("w", 2), ("w", 3)]]
 HEAD_WINDOWS = (0,)
 HEAD_ENGINES = ("s", "s", "s")
-IN_LEAD = 8
+IN_LEAD = 7
 ONE_ONE = 1.0019454956054688
 KICK = 9
 KICK_HEAD = 4

@@ -28,7 +28,7 @@ GROUP = {6: 5}
 HEAD_STAGES = [[("w", 0), ("w", 1)], [("x", 0, 0), ("x", 0, 1)], [("w", 2), ("w", 3)]]
 HEAD_WINDOWS = (0,)
 HEAD_ENGINES = ("s", "s", "s")
-IN_LEAD = 7
+IN_LEAD = {1: 7, 2: 5, 3: 6, 4: 7, 5: 7}
 ONE_ONE = 1.0019454956054688
 KICK = 9
 KICK_HEAD = 4
@@ -375,7 +375,7 @@ def tile_cvim_pa_kernel(tc, x, w1, b1, w2, b2, out_0, out_1):
         early = {}
         for i in range(NW):
             if i not in HEAD_WINDOWS and i not in GROUP:
-                early.setdefault(max(first, ND * i - IN_LEAD), []).append(i)
+                early.setdefault(max(first, ND * i - IN_LEAD[i]), []).append(i)
         late = {}
         done = {0: 0, 1: 0}
         n_out = [0]

@@ -51,8 +51,8 @@ def tile_cvim_pa_kernel(tc, x, w1, b1, w2, b2, out_0, out_1):
 
     with ExitStack() as ctx:
         const = ctx.enter_context(tc.tile_pool(name="const", bufs=1))
-        grp = ctx.enter_context(tc.tile_pool(name="grp", bufs=3))
-        res = ctx.enter_context(tc.tile_pool(name="res", bufs=6))
+        grp = ctx.enter_context(tc.tile_pool(name="grp", bufs=8))
+        res = ctx.enter_context(tc.tile_pool(name="res", bufs=16))
         psum = ctx.enter_context(tc.psum_pool(name="psum", bufs=8))
 
         w2_b = const.tile([P, ND, KW], BF16, name="w2_b")

from contextlib import ExitStack

import concourse.mybir as mybir
from concourse.masks import make_identity

B, T, C, D, KW = 2, 1024, 512, 512, 3
Y_SCALE = 140.0
FLOPS = 2 * B * T * C * D + 2 * KW * B * T * D

F32 = mybir.dt.float32
BF16 = mybir.dt.bfloat16
U32 = mybir.dt.uint32
U8 = mybir.dt.uint8
FP8X4 = mybir.dt.float8_e4m3fn_x4
FP8 = mybir.dt.float8_e4m3fn
ALU = mybir.AluOpType
ACT = mybir.ActivationFunctionType
AX = mybir.AxisListType

P = 128
ND = D // P
WORDS = C // 2

WINDOWS = [(0, 0, 256), (0, 256, 256), (0, 512, 512), (1, 0, 512), (1, 512, 256), (1, 768, 128), (1, 896, 128)]
PAIRED = (0, 1, 4)
JOINED_LOADS = {3: (4, 5)}
GROUP = {6: 5}
HEAD_STAGES = [[("w", 0), ("w", 1)], [("x", 0, 0), ("x", 0, 1)], [("w", 2), ("w", 3)]]
HEAD_WINDOWS = (0,)
HEAD_ENGINES = ("s", "s", "s")
IN_LEAD = {1: 7, 2: 5, 3: 6, 4: 7, 5: 7}
ONE_ONE = 1.0019454956054688
KICK = 9
KICK_HEAD = 4
KICK_TAIL = 0
MM_LEAD = {512: 1, 256: 2, 128: 2}
QUANT_LAG = 1
OUT_LEAD = 1
SCALAR_CASTS = (5, 13)
DIAG_UNITS = ((1, 3), (2, 3))
VECTOR_COPIES = ()
BYTES_GROUPS = ((0, 1, 2), (3, 4, 5, 6), (8, 9, 10), (11, 12), (13, 14))
LAST_PARTS = ((0, 2), (2, 4))


def tile_cvim_pa_kernel(tc, x, w1, b1, w2, b2, out_0, out_1):
    nc = tc.nc
    o0 = out_0.flatten_outer_dims()
    o1 = out_1.flatten_outer_dims()
    NW = len(WINDOWS)

    with ExitStack() as ctx:
        const = ctx.enter_context(tc.tile_pool(name="const", bufs=1))
        grp = ctx.enter_context(tc.tile_pool(name="grp", bufs=8))
        res = ctx.enter_context(tc.tile_pool(name="res", bufs=16))
        psum = ctx.enter_context(tc.psum_pool(name="psum", bufs=8))

        w2_b = const.tile([P, ND, KW], BF16, name="w2_b")
        b1_b = const.tile([P, ND], BF16, name="b1_b")
        b2_b = const.tile([P, ND], BF16, name="b2_b")

        w_view = w1.rearrange("(h p l) c -> h p l c", h=2, l=2)
        w_raw = {}
        x_raw = {}

        def load_w(j0, j1):
            wr = const.tile([P, j1 - j0, C], BF16, name="w_raw%d" % j0)
            nc.sync.dma_start(out=wr[:], in_=w_view[j0 // 2])
            for j in range(j0, j1):
                w_raw[j] = wr[:, j - j0, :]

        def span(i):
            return WINDOWS[i][2] + sum([WINDOWS[f][2] for f in GROUP if GROUP[f] == i])

        def load_x(i):
            b, t0, n = WINDOWS[i]
            members = [i] + [f for f in JOINED_LOADS.get(i, ())]
            n = sum([span(f) for f in members])
            xr = const.tile([P, n // P, C], BF16, name="x_raw%d" % i)
            nc.sync.dma_start(out=xr[:], in_=x[b, t0 : t0 + n, :].rearrange("(n p) c -> p n c", p=P))
            slot = 0
            for f in members:
                x_raw[f] = xr[:, slot : slot + span(f) // P, :]
                slot += span(f) // P

        load_w(0, 2)
        load_x(0)
        with nc.allow_non_contiguous_dma(reason="one value of a 512-long vector to a partition"):
            nc.sync.dma_start(out=w2_b[:].rearrange("p (h l) k -> p h (l k)", h=2), in_=w2.rearrange("(h p l) k -> p h (l k)", h=2, l=2))
            nc.sync.dma_start(out=b1_b[:].rearrange("p (h l) -> p h l", h=2), in_=b1.rearrange("(h p l) -> p h l", h=2, l=2))
            nc.sync.dma_start(out=b2_b[:].rearrange("p (h l) -> p h l", h=2), in_=b2.rearrange("(h p l) -> p h l", h=2, l=2))
        load_w(2, 4)
        for i in range(1, NW):
            if i not in GROUP and not any([i in JOINED_LOADS[f] for f in JOINED_LOADS]):
                load_x(i)

        warm = const.tile([P, 1], F32, name="warm")
        nc.vector.memset(warm[:], 0.0)
        nc.scalar.activation(out=warm[:], in_=warm[:], func=ACT.Identity)

        ones = const.tile([P, 512], BF16, name="ones", align_bytes=64)
        ones_codes = const.tile([P, P], U32, name="ones_codes", align_bytes=64)
        ones_scales = const.tile([P, P], U8, name="ones_scales", align_bytes=64)
        nc.vector.memset(ones[:].bitcast(F32), ONE_ONE)
        nc.vector.quantize_mx(out=ones_codes[:].bitcast(FP8X4), scales=ones_scales[:], in_=ones[:])
        idle = psum.tile([P, 512], F32, name="bank")

        def kick(times, bank=idle):
            for r in range(times):
                nc.tensor.matmul_mx(
                    out=bank[:, 0:P], lhsT=ones_codes[:].bitcast(FP8X4), lhsT_scale=ones_scales[:],
                    rhs=ones_codes[:].bitcast(FP8X4), rhs_scale=ones_scales[:], start=True, stop=True,
                )

        kick(KICK)

        ident = const.tile([P, P], F32, name="ident")
        make_identity(nc, ident[:])

        taps = const.tile([P, ND, KW], F32, name="taps")
        nc.vector.tensor_copy(out=taps[:], in_=w2_b[:])
        beta = const.tile([P, ND], F32, name="beta")
        beta_first = const.tile([P, ND], F32, name="beta_first")
        edge0 = const.tile([P, ND], F32, name="edge0")
        edge2 = const.tile([P, ND], F32, name="edge2")
        nc.vector.tensor_reduce(out=beta[:], in_=taps[:], op=ALU.add, axis=AX.X)
        nc.vector.tensor_tensor(out=edge0[:], in0=taps[:, :, 0], in1=b1_b[:], op=ALU.mult)
        nc.vector.tensor_tensor(out=beta[:], in0=beta[:], in1=b1_b[:], op=ALU.mult)
        nc.vector.tensor_tensor(out=edge2[:], in0=taps[:, :, 2], in1=b1_b[:], op=ALU.mult)
        nc.vector.tensor_tensor(out=beta[:], in0=beta[:], in1=b2_b[:], op=ALU.add)
        nc.vector.tensor_tensor(out=beta_first[:], in0=beta[:], in1=edge0[:], op=ALU.subtract)

        y = []
        for b in range(B):
            yb = const.tile([P, ND, T], F32, name="y%d" % b)
            nc.vector.tensor_copy(out=yb[:, :, 0:1], in_=beta_first[:].unsqueeze(2))
            y.append(yb)

        def beside(i, step):
            e = i + step
            return e if 0 <= e < NW and WINDOWS[e][0] == WINDOWS[i][0] else None

        hpad = {}
        for b, j in sorted(set([(WINDOWS[i][0], j) for i, j in DIAG_UNITS])):
            hp = const.tile([P, T + 2], F32, name="hpad%d_%d" % (b, j))
            nc.vector.memset(hp[:, 0:1], 0.0)
            nc.vector.memset(hp[:, T + 1 : T + 2], 0.0)
            hpad[(b, j)] = hp
        b1_f = const.tile([P, ND], F32, name="b1_f")
        nc.vector.tensor_copy(out=b1_f[:], in_=b1_b[:])
        diag = {}
        b2_rep = {}
        for j in sorted(set([u[1] for u in DIAG_UNITS])):
            dg = const.tile([P, KW, P], F32, name="diag%d" % j)
            for r in range(KW):
                nc.vector.tensor_scalar(out=dg[:, r, :], in0=ident[:], scalar1=taps[:, j, r : r + 1], scalar2=None, op0=ALU.mult)
            br = const.tile([P, P], F32, name="b2_rep%d" % j)
            nc.vector.tensor_copy(out=br[:], in_=b2_b[:, j : j + 1].to_broadcast([P, P]))
            diag[j] = dg
            b2_rep[j] = br

        def to_mx(slots, name, engine):
            nt = len(slots)
            codes = const.tile([P, nt * P], U32, name="codes_" + name, align_bytes=64)
            scales = const.tile([P, nt * P], U8, name="scales_" + name, align_bytes=64)
            grouped = grp.tile([P, nt * P * 4], BF16, name="grouped", align_bytes=64)
            g_words = grouped[:].bitcast(F32)
            for h in range(0, nt, 2):
                na = min(2, nt - h)
                bank = psum.tile([P, 512], F32, name="bank")
                turned = bank[:].rearrange("p (a u r) -> p a u r", a=2, u=2)
                for a in range(na):
                    for u in range(2):
                        nc.tensor.transpose(out=turned[:, a, u, :], in_=slots[h + a][:, u:WORDS:2], identity=ident[:])
                dst = g_words[:, 2 * P * h : 2 * P * (h + na)].rearrange("p (a r u) -> p a r u", a=na, u=2)
                if engine == "v":
                    nc.vector.tensor_copy(out=dst, in_=turned[:, 0:na].rearrange("p a u r -> p a r u"))
                else:
                    nc.scalar.copy(out=dst, in_=turned[:, 0:na].rearrange("p a u r -> p a r u"))
            def quantise():
                nc.vector.quantize_mx(out=codes[:].bitcast(FP8X4), scales=scales[:], in_=grouped[:])

            return codes, scales, quantise

        w_mx = {}
        x_mx = {}

        def stage_head(q):
            slots = []
            for item in HEAD_STAGES[q]:
                if item[0] == "w":
                    slots.append(w_raw[item[1]].bitcast(F32))
                else:
                    slots.append(x_raw[item[1]][:, item[2], :].bitcast(F32))
            codes, scales, quantise = to_mx(slots, "h%d" % q, HEAD_ENGINES[q])
            quantise()
            for a, item in enumerate(HEAD_STAGES[q]):
                cols = slice(a * P, (a + 1) * P)
                if item[0] == "w":
                    w_mx[item[1]] = (codes[:, cols], scales[:, cols])
                elif item[2] == 0:
                    n = WINDOWS[item[1]][2]
                    x_mx[item[1]] = (codes[:, a * P : a * P + n], scales[:, a * P : a * P + n])

        def stage_in(i):
            n = span(i)
            xw = x_raw[i][:].bitcast(F32)
            codes, scales, quantise = to_mx([xw[:, a, :] for a in range(n // P)], "x%d" % i, "s")
            x_mx[i] = (codes[:], scales[:])
            return quantise

        units = [(i, j) for i in range(NW) for j in range(ND)]
        NU = len(units)
        accs = {}

        def unit_mm(s):
            i, j = units[s]
            n = span(i)
            x_codes, x_scales = x_mx[i]
            bank = psum.tile([P, 512], F32, name="bank")
            for e in range(2 if i in PAIRED else 1):
                w_codes, w_scales = w_mx[j + e]
                nc.tensor.matmul_mx(
                    out=bank[:, e * n : (e + 1) * n],
                    lhsT=w_codes.bitcast(FP8X4),
                    lhsT_scale=w_scales,
                    rhs=x_codes.bitcast(FP8X4),
                    rhs_scale=x_scales,
                    start=True,
                    stop=True,
                )
                accs[s + e] = bank[:, e * n : e * n + WINDOWS[i][2] + (1 if n > WINDOWS[i][2] else 0)]
            off = WINDOWS[i][2]
            for f in sorted(GROUP):
                if GROUP[f] == i:
                    accs[s + ND * (f - i)] = bank[:, off : off + WINDOWS[f][2]]
                    off += WINDOWS[f][2]

        def unit_prev(s):
            i, j = units[s]
            b, t0, n = WINDOWS[i]
            before, after = beside(i, -1), beside(i, 1)
            if (i, j) in DIAG_UNITS:
                nc.scalar.activation(
                    out=hpad[(b, j)][:, 1 + t0 : 1 + t0 + n], in_=accs[s][:, 0:n], func=ACT.Identity,
                    bias=b1_f[:, j : j + 1], scale=1.0,
                )
                if after is not None and (after, j) not in DIAG_UNITS:
                    nc.scalar.activation(
                        out=y[b][:, j, t0 + n : t0 + n + 1], in_=accs[s][:, n - 1 : n], func=ACT.Identity,
                        bias=beta[:, j : j + 1], scale=taps[:, j, 0:1],
                    )
                return
            if before is not None and (before, j) in DIAG_UNITS:
                nc.scalar.activation(
                    out=hpad[(b, j)][:, 1 + t0 : 2 + t0], in_=accs[s][:, 0:1], func=ACT.Identity,
                    bias=b1_f[:, j : j + 1], scale=1.0,
                )
            m = n if t0 + n < T else n - 1
            if after is not None and (after, j) in DIAG_UNITS:
                nc.scalar.activation(
                    out=hpad[(b, j)][:, t0 + n : t0 + n + 1], in_=accs[s][:, n - 1 : n], func=ACT.Identity,
                    bias=b1_f[:, j : j + 1], scale=1.0,
                )
                m = n - 1
            nc.scalar.activation(
                out=y[b][:, j, t0 + 1 : t0 + 1 + m], in_=accs[s][:, 0:m], func=ACT.Identity,
                bias=beta[:, j : j + 1], scale=taps[:, j, 0:1],
            )

        def unit_mid(s):
            i, j = units[s]
            b, t0, n = WINDOWS[i]
            if (i, j) in DIAG_UNITS:
                return
            yj = y[b][:, j, :]
            nc.vector.scalar_tensor_tensor(
                out=yj[:, t0 : t0 + n], in0=accs[s][:, 0:n], scalar=taps[:, j, 1:2], in1=yj[:, t0 : t0 + n],
                op0=ALU.mult, op1=ALU.add,
            )

        def unit_next(s):
            i, j = units[s]
            b, t0, n = WINDOWS[i]
            before = beside(i, -1)
            yj = y[b][:, j, :]
            lo = 1 if t0 == 0 or i in GROUP or (before, j) in DIAG_UNITS else 0
            hi = n + 1 if i + 1 in GROUP else n
            if (i, j) in DIAG_UNITS:
                if before is None or (before, j) in DIAG_UNITS:
                    return
                hi = 1
            nc.vector.scalar_tensor_tensor(
                out=yj[:, t0 + lo - 1 : t0 + hi - 1], in0=accs[s][:, lo:hi], scalar=taps[:, j, 2:3],
                in1=yj[:, t0 + lo - 1 : t0 + hi - 1], op0=ALU.mult, op1=ALU.add,
            )

        def last_column(b):
            nj = min([ND] + [j for i, j in DIAG_UNITS if WINDOWS[i][0] == b and WINDOWS[i][1] + WINDOWS[i][2] == T])
            col = y[b][:, 0:nj, T - 1 : T]
            nc.vector.tensor_tensor(out=col, in0=col, in1=edge2[:, 0:nj].unsqueeze(2), op=ALU.subtract)

        shared = {}

        def tile_out(b, k, n, by_scalar, by_vector, cast_later):
            rows = slice(b * T + k * P, b * T + (k + 1) * P)
            r32 = res.tile([P, D], F32, name="r32")
            group = ([g for g in BYTES_GROUPS if n in g] + [(n,)])[0]
            q = group.index(n)
            if q == 0:
                r8_new = res.tile([P, len(group), D], FP8, name="r8")
                shared["r8"] = r8_new
            r8g = shared["r8"]
            group_rows = slice(b * T + (k - q) * P, b * T + (k - q + len(group)) * P)
            last = b == B - 1 and k == T // P - 1
            parts = LAST_PARTS if last else ((0, ND),)
            for j0, j1 in parts:
                bank = psum.tile([P, 512], F32, name="bank")
                if b == B - 1 and k >= T // P - 4 and j0 == 0:
                    kick(KICK_TAIL, bank)
                for j in range(j0, j1):
                    if by_scalar:
                        there = bank[:, 2 * P * (j // 2) + j % 2 : 2 * P * (j // 2 + 1) : 2]
                    else:
                        there = bank[:, (j - j0) * P : (j - j0 + 1) * P]
                    home = [i for i in range(NW) if WINDOWS[i][0] == b and WINDOWS[i][1] <= k * P < WINDOWS[i][1] + WINDOWS[i][2]][0]
                    if (home, j) in DIAG_UNITS:
                        c0 = k * P
                        nc.tensor.matmul(out=there, lhsT=b2_rep[j][:], rhs=ident[:], is_transpose=True, start=True, stop=False)
                        for r in range(KW):
                            nc.tensor.matmul(
                                out=there, lhsT=hpad[(b, j)][:, c0 + r : c0 + P + r], rhs=diag[j][:, r, :],
                                start=False, stop=(r == KW - 1),
                            )
                    else:
                        nc.tensor.transpose(out=there, in_=y[b][:, j, k * P : (k + 1) * P], identity=ident[:])
                cols = slice(j0 * P, j1 * P)
                turned = bank[:, 0 : (j1 - j0) * P]
                if by_scalar:
                    nc.scalar.copy(out=r32[:, cols], in_=turned)
                else:
                    nc.scalar.copy(
                        out=r32[:, cols].rearrange("t (h p l) -> t h p l", p=P, l=2),
                        in_=turned.rearrange("t (h l p) -> t h p l", p=P, l=2),
                    )
                if j1 == ND:
                    nc.sync.dma_start(out=o0[rows, :], in_=r32[:])
                whole = q == len(group) - 1 and j1 == ND

                def cast(cols=cols, turned=turned, whole=whole):
                    if by_scalar:
                        nc.scalar.activation(out=r8g[:, q, cols], in_=turned, func=ACT.Copy, scale=Y_SCALE, saturate=False)
                    else:
                        nc.vector.tensor_scalar(out=r8g[:, q, cols], in0=r32[:, cols], scalar1=Y_SCALE, scalar2=None, op0=ALU.mult, saturate=False)
                    if whole:
                        nc.sync.dma_start(out=o1[group_rows, :].rearrange("(q p) d -> p q d", p=P), in_=r8g[:].bitcast(U8))

                if by_scalar:
                    cast()
                else:
                    cast_later(cast)

        mm_at = {}
        prev_at = {}
        for u in range(NU):
            if units[u][0] in PAIRED:
                if units[u][1] % 2 == 0:
                    mm_at.setdefault(u - 3, []).append(u)
                prev_at.setdefault(u - 2, []).append(u)
            else:
                if units[u][0] not in GROUP:
                    mm_at.setdefault(u - MM_LEAD[span(units[u][0])], []).append(u)
                prev_at.setdefault(u - 1, []).append(u)
        first = min(mm_at)
        early = {}
        for i in range(NW):
            if i not in HEAD_WINDOWS and i not in GROUP:
                early.setdefault(max(first, ND * i - IN_LEAD[i]), []).append(i)
        late = {}
        done = {0: 0, 1: 0}
        n_out = [0]

        for q in range(len(HEAD_STAGES)):
            stage_head(q)
            if q < len(HEAD_STAGES) - 1:
                kick(KICK_HEAD)
        for s in range(first, NU + 16):
            for i in early.get(s, []):
                late.setdefault(s + QUANT_LAG, []).append((stage_in(i),))
            for u in mm_at.get(s, []):
                unit_mm(u)
            for u in prev_at.get(s, []):
                unit_prev(u)
            if 0 <= s < NU:
                i, j = units[s]
                b, t0, n = WINDOWS[i]
                if i == NW - 1:
                    unit_next(s)
                    if j == ND - 1:
                        for r, k in enumerate(range(done[b], t0 // P)):
                            late.setdefault(s + OUT_LEAD + r, []).append((b, k))
                        done[b] = t0 // P
                else:
                    unit_mid(s)
            if 0 <= s - 1 < NU:
                i, j = units[s - 1]
                b, t0, n = WINDOWS[i]
                if j == ND - 1 and t0 + n == T:
                    last_column(b)
                if i == NW - 1:
                    unit_mid(s - 1)
                else:
                    unit_next(s - 1)
                if j == ND - 1:
                    ready = T // P if t0 + n == T else ((t0 + n) // P if i + 1 in GROUP else (t0 + n - 1) // P)
                    for r, k in enumerate(range(done[b], ready)):
                        late.setdefault(s + OUT_LEAD + r, []).append((b, k))
                    done[b] = ready
            for item in late.get(s, []):
                if len(item) == 1:
                    item[0]()
                else:
                    b, k = item
                    by_scalar = n_out[0] in SCALAR_CASTS
                    by_vector = n_out[0] in VECTOR_COPIES
                    n_out[0] += 1
                    tile_out(b, k, n_out[0] - 1, by_scalar, by_vector, lambda fn: late.setdefault(s + 1, []).append((fn,)))
